import numpy as np
import ml_dtypes


def mxq(x, axis, fmt="e4m3"):
    dtype, down = {"e4m3": (ml_dtypes.float8_e4m3fn, 7), "e5m2": (ml_dtypes.float8_e5m2, 14)}[fmt]
    v = np.moveaxis(np.asarray(x, np.float32).astype(ml_dtypes.bfloat16).astype(np.float64), axis, -1)
    blocks = v.reshape(v.shape[:-1] + (-1, 32))
    amax = np.abs(blocks).max(-1, keepdims=True)
    byte = np.maximum(np.where(amax > 0, np.frexp(amax)[1] - 1 + 127, 0) - down, 1)
    scale = np.exp2(byte - 127.0)
    codes = (blocks / scale).astype(np.float32).astype(dtype).astype(np.float64)
    return np.moveaxis((codes * scale).reshape(v.shape), -1, axis)


WIDE = False


def mx_kscale(k):
    if not WIDE:
        return np.ones(k)
    levels = np.array([20, -20, 10, -10, 0])
    a = np.random.permutation(np.resize(levels, k // 512 * 4)).reshape(k // 512, 4)
    idx = np.arange(k)
    return np.exp2(a[idx // 512, idx % 128 // 32])


BF16 = ml_dtypes.bfloat16


def bf(x):
    return np.asarray(x, np.float32).astype(BF16)


def f64(x):
    return np.asarray(x).astype(np.float64)


B, I, O, G = 512, 128, 8192, 8
K = I * G


def bspline_basis(d):
    inner = 1.0 - 6.0 * d * d + 6.0 * d * d * d
    outer = 2.0 * (1.0 - d) ** 3
    return np.where(d < 0.5, inner, np.where(d < 1.0, outer, np.zeros_like(d)))


def bspline_slope(d):
    inner = -12.0 * d + 18.0 * d * d
    outer = -6.0 * (1.0 - d) ** 2
    return np.where(d < 0.5, inner, np.where(d < 1.0, outer, np.zeros_like(d)))


def setup_inputs():
    g = np.linspace(-1.0, 1.0, G)
    s = mx_kscale(O)
    x_norm = np.tanh(np.random.standard_normal((B, I)))
    spline_weight = np.random.standard_normal((O, I, G)) / np.sqrt(I) / s[:, None, None]
    base_activation = np.random.standard_normal((O, I)) * 4.0 / np.sqrt(I) / s[:, None]
    grid_points = g + 0.1 * (g[1] - g[0]) * np.random.standard_normal(G)
    grad_out = np.random.standard_normal((B, O)) * np.exp2(np.random.randint(-12, 1, (B, 1))) * 4.0 * s
    return {"x_norm": bf(x_norm),
            "spline_weight": bf(spline_weight),
            "base_activation": bf(base_activation),
            "grid_points": bf(grid_points),
            "grad_out": bf(grad_out)}


def reference(x_norm, spline_weight, base_activation, grid_points, grad_out):
    t = f64(x_norm)
    diff = t[:, :, None] - f64(grid_points)
    slope = bspline_slope(np.abs(diff)) * np.sign(diff)
    gq = mxq(f64(grad_out), 1, "e5m2")
    h = gq @ mxq(f64(spline_weight).reshape(O, K), 0, "e4m3")
    base = gq @ mxq(f64(base_activation), 0, "e4m3")
    return (h.reshape(B, I, G) * slope).sum(axis=2) + 0.1 * base

@@ -1,0 +1,256 @@
+from contextlib import ExitStack
+
+import concourse.mybir as mybir
+from concourse.masks import make_identity
+
+F32 = mybir.dt.float32
+BF16 = mybir.dt.bfloat16
+U32 = mybir.dt.uint32
+U8 = mybir.dt.uint8
+E4M3_X4 = mybir.dt.float8_e4m3fn_x4
+E5M2_X4 = mybir.dt.float8_e5m2_x4
+ALU = mybir.AluOpType
+ACT = mybir.ActivationFunctionType
+AXIS_X = mybir.AxisListType.X
+
+P = 128
+PACK = 4
+K_PASS = P * PACK
+
+B, I, O, G = 512, 128, 8192, 8
+COLS = I * G
+PASSES = O // K_PASS
+GROUPS = COLS // P
+FEATS = P // G
+ROW_TILES = B // P
+BLOCK_PASSES = 4
+BASE_PASSES = COLS // I
+RUN = 4
+VECTOR_COLS = 576
+
+FLOPS = 2 * B * O * (COLS + I)
+
+
+def tile_advancedkanlayer_pa_k_kernel(
+    tc, x_norm, spline_weight, base_activation, grid_points, grad_out, out
+):
+    nc = tc.nc
+    with ExitStack() as ctx:
+        const = ctx.enter_context(tc.tile_pool(name="const", bufs=1))
+        keep = ctx.enter_context(tc.tile_pool(name="keep", bufs=1))
+        stream = ctx.enter_context(tc.tile_pool(name="stream", bufs=2))
+        psum = ctx.enter_context(tc.psum_pool(name="psum", bufs=1))
+
+        def bank(n, shape, dtype, name):
+            return psum.tile(shape, dtype, tag="bank%d" % n, name=name)
+
+        x_rows = const.tile([P, ROW_TILES, I], BF16)
+        nc.sync.dma_start(out=x_rows[:], in_=x_norm.rearrange("(r p) i -> p r i", p=P))
+        knots = const.tile([P, G], BF16)
+        nc.sync.dma_start(out=knots[:], in_=grid_points.partition_broadcast(P))
+
+        ident_f32 = const.tile([P, P], F32)
+        make_identity(nc, ident_f32[:])
+        ident_bf16 = const.tile([P, P], BF16)
+        make_identity(nc, ident_bf16[:])
+
+        spread = const.tile([P, COLS], BF16)
+        nc.vector.tensor_copy(
+            out=spread[:].rearrange("p (i g) -> p i g", g=G),
+            in_=ident_bf16[:].unsqueeze(2).to_broadcast([P, P, G]),
+        )
+        same_feature = const.tile([P, FEATS], F32)
+        nc.vector.tensor_reduce(
+            out=same_feature[:],
+            in_=ident_f32[:].rearrange("p (j g) -> p j g", g=G),
+            axis=AXIS_X,
+            op=ALU.add,
+        )
+        gather = const.tile([P, GROUPS, I], F32)
+        nc.vector.memset(gather[:], 0.0)
+        for n in range(GROUPS):
+            nc.vector.tensor_copy(
+                out=gather[:, n, FEATS * n : FEATS * (n + 1)], in_=same_feature[:]
+            )
+        same_knot = const.tile([P, G], F32)
+        nc.vector.tensor_reduce(
+            out=same_knot[:],
+            in_=ident_f32[:].rearrange("p (j g) -> p g j", g=G),
+            axis=AXIS_X,
+            op=ALU.add,
+        )
+        own_knot = const.tile([P, G], F32)
+        nc.vector.tensor_tensor(out=own_knot[:], in0=same_knot[:], in1=knots[:], op=ALU.mult)
+        knot = const.tile([P, 1], F32)
+        nc.vector.tensor_reduce(out=knot[:], in_=own_knot[:], axis=AXIS_X, op=ALU.add)
+        neg_knot = const.tile([P, 1], F32)
+        nc.vector.tensor_scalar_mul(out=neg_knot[:], in0=knot[:], scalar1=-1.0)
+
+        xT_bank = bank(7, [P, B], BF16, "xT_bank")
+        for r in range(ROW_TILES):
+            nc.tensor.transpose(
+                out=xT_bank[:, P * r : P * (r + 1)], in_=x_rows[:, r, :], identity=ident_bf16[:]
+            )
+        xT = const.tile([P, B], BF16)
+        nc.vector.tensor_copy(out=xT[:], in_=xT_bank[:])
+
+        slope = keep.tile([P, GROUPS, B], F32)
+        dist = []
+        for n in range(GROUPS):
+            x_spread = bank(4 + n % 3, [P, B], F32, "x_spread")
+            nc.tensor.matmul(
+                out=x_spread[:], lhsT=spread[:, P * n : P * (n + 1)], rhs=xT[:], start=True, stop=True
+            )
+            d = keep.tile([P, B], F32, tag="dist", bufs=GROUPS, name="d")
+            nc.scalar.activation(out=d[:], in_=x_spread[:], func=ACT.Abs, bias=neg_knot[:], scale=1.0)
+            nc.scalar.activation(
+                out=slope[:, n, :], in_=x_spread[:], func=ACT.Sign, bias=neg_knot[:], scale=1.0
+            )
+            dist.append(d)
+
+        g_codes = keep.tile([P, PASSES, B], U32, align_bytes=64)
+        g_scales = keep.tile([P, PASSES, B], U8, align_bytes=64)
+        block_cols = BLOCK_PASSES * K_PASS
+        for blk in range(PASSES // BLOCK_PASSES):
+            g_rows = stream.tile([P, ROW_TILES * block_cols], BF16, tag="g_rows", bufs=2)
+            nc.sync.dma_start(
+                out=g_rows[:].rearrange("p (r o) -> p r o", r=ROW_TILES),
+                in_=grad_out[:, block_cols * blk : block_cols * (blk + 1)].rearrange(
+                    "(r p) o -> p r o", p=P
+                ),
+            )
+            g_words = g_rows[:].bitcast(F32).rearrange("p (r w) -> p r w", r=ROW_TILES)
+            for c in range(BLOCK_PASSES * blk, BLOCK_PASSES * (blk + 1)):
+                first_word = (K_PASS // 2) * (c % BLOCK_PASSES)
+                g_grouped = stream.tile([P, B * PACK], BF16, tag="g_grouped", bufs=3, align_bytes=64)
+                g_grouped_words = g_grouped[:].bitcast(F32).rearrange("p (b u) -> p b u", u=2)
+                for half in range(2):
+                    flipped = bank((2 * c + half) % 4, [P, 2, B // 2], F32, "flipped")
+                    for u in range(2):
+                        for r in range(2):
+                            nc.tensor.transpose(
+                                out=flipped[:, u, P * r : P * (r + 1)],
+                                in_=g_words[
+                                    :, 2 * half + r, first_word + P * u : first_word + P * (u + 1)
+                                ],
+                                identity=ident_f32[:],
+                            )
+                    nc.scalar.copy(
+                        out=g_grouped_words[:, (B // 2) * half : (B // 2) * (half + 1), :],
+                        in_=flipped[:].rearrange("p u b -> p b u"),
+                    )
+                nc.vector.quantize_mx(
+                    out=g_codes[:, c, :].bitcast(E5M2_X4), scales=g_scales[:, c, :], in_=g_grouped[:]
+                )
+
+        def regroup(raw):
+            grouped = stream.tile([P, COLS, PACK], BF16, tag="w_grouped", bufs=2, align_bytes=64)
+            src = raw[:].rearrange("p t (c i) -> p c t i", i=RUN)
+            dst = grouped[:].rearrange("p (c i) t -> p c t i", i=RUN)
+            cut = VECTOR_COLS // RUN
+            nc.vector.tensor_copy(out=dst[:, :cut], in_=src[:, :cut])
+            nc.scalar.copy(out=dst[:, cut:], in_=src[:, cut:])
+            return grouped
+
+        def quantise(grouped, codes, scales):
+            nc.vector.quantize_mx(
+                out=codes.bitcast(E4M3_X4),
+                scales=scales,
+                in_=grouped[:].rearrange("p w t -> p (w t)"),
+            )
+
+        base_rows = base_activation.rearrange(
+            "(c u p e) i -> u e p c i", c=PASSES, u=2, p=P, e=2
+        )
+        base_bank = bank(7, [P, B], F32, "base_bank")
+        for chunk in range(PASSES // BASE_PASSES):
+            passes = range(BASE_PASSES * chunk, BASE_PASSES * (chunk + 1))
+            raw = stream.tile([P, PACK, COLS], BF16, tag="w_raw", bufs=4, name="base_raw")
+            for u in range(2):
+                for e in range(2):
+                    nc.sync.dma_start(
+                        out=raw[:, 2 * u + e, :].rearrange("p (c i) -> p c i", i=I),
+                        in_=base_rows[u, e][:, passes[0] : passes[0] + BASE_PASSES, :],
+                    )
+            b_codes = keep.tile([P, COLS], U32, tag="b_codes", bufs=2, align_bytes=64)
+            b_scales = keep.tile([P, COLS], U8, tag="b_scales", bufs=2, align_bytes=64)
+            quantise(regroup(raw), b_codes[:], b_scales[:])
+            for c in passes:
+                cols = slice(I * (c % BASE_PASSES), I * (c % BASE_PASSES + 1))
+                nc.tensor.matmul_mx(
+                    out=base_bank[:],
+                    lhsT=b_codes[:, cols].bitcast(E4M3_X4),
+                    lhsT_scale=b_scales[:, cols],
+                    rhs=g_codes[:, c, :].bitcast(E5M2_X4),
+                    rhs_scale=g_scales[:, c, :],
+                    start=(c == 0),
+                    stop=(c == PASSES - 1),
+                )
+        base_part = keep.tile([P, B], F32)
+        nc.scalar.mul(out=base_part[:], in_=base_bank[:], mul=0.1)
+
+        for n in range(GROUPS):
+            d = dist[n]
+            outer = keep.tile([P, B], F32, tag="outer", bufs=2)
+            nc.vector.tensor_scalar(
+                out=outer[:], in0=d[:], scalar1=1.0, scalar2=1.0, op0=ALU.min, op1=ALU.subtract
+            )
+            nc.vector.tensor_scalar(
+                out=d[:], in0=d[:], scalar1=0.5, scalar2=0.5, op0=ALU.min, op1=ALU.subtract
+            )
+            nc.scalar.square(out=outer[:], in_=outer[:])
+            nc.scalar.square(out=d[:], in_=d[:])
+            nc.vector.scalar_tensor_tensor(
+                out=d[:], in0=d[:], scalar=4.0, in1=outer[:], op0=ALU.mult, op1=ALU.subtract
+            )
+            nc.vector.tensor_tensor(out=slope[:, n, :], in0=d[:], in1=slope[:, n, :], op=ALU.mult)
+
+        w_rows = spline_weight.rearrange(
+            "(c u p e) i g -> c p u (e i g)", c=PASSES, u=2, p=P, e=2
+        )
+        h = [bank(n, [P, B], F32, "h%d" % n) for n in range(GROUPS)]
+        for c in range(PASSES):
+            raw = stream.tile([P, PACK, COLS], BF16, tag="w_raw", bufs=4, name="w_raw")
+            nc.sync.dma_start(
+                out=raw[:].rearrange("p (u e) w -> p u (e w)", u=2), in_=w_rows[c]
+            )
+            w_codes = stream.tile([P, COLS], U32, tag="w_codes", bufs=4, align_bytes=64)
+            w_scales = stream.tile([P, COLS], U8, tag="w_scales", bufs=4, align_bytes=64)
+            quantise(regroup(raw), w_codes[:], w_scales[:])
+            for n in range(GROUPS):
+                cols = slice(P * n, P * (n + 1))
+                nc.tensor.matmul_mx(
+                    out=h[n][:],
+                    lhsT=w_codes[:, cols].bitcast(E4M3_X4),
+                    lhsT_scale=w_scales[:, cols],
+                    rhs=g_codes[:, c, :].bitcast(E5M2_X4),
+                    rhs_scale=g_scales[:, c, :],
+                    start=(c == 0),
+                    stop=(c == PASSES - 1),
+                )
+
+        spline_bank = None
+        for n in range(GROUPS):
+            weighted = stream.tile([P, B], F32, tag="weighted", bufs=3)
+            nc.vector.scalar_tensor_tensor(
+                out=weighted[:], in0=h[n][:], scalar=6.0, in1=slope[:, n, :], op0=ALU.mult, op1=ALU.mult
+            )
+            if n == 0:
+                spline_bank = bank(0, [P, B], F32, "spline_bank")
+            nc.tensor.matmul(
+                out=spline_bank[:],
+                lhsT=gather[:, n, :],
+                rhs=weighted[:],
+                start=(n == 0),
+                stop=(n == GROUPS - 1),
+            )
+        outT = keep.tile([P, B], F32)
+        nc.vector.tensor_tensor(out=outT[:], in0=spline_bank[:], in1=base_part[:], op=ALU.add)
+        out_bank = bank(1, [P, ROW_TILES, I], F32, "out_bank")
+        for r in range(ROW_TILES):
+            nc.tensor.transpose(
+                out=out_bank[:, r, :], in_=outT[:, P * r : P * (r + 1)], identity=ident_f32[:]
+            )
+        out_rows = keep.tile([P, ROW_TILES, I], F32)
+        nc.vector.tensor_copy(out=out_rows[:], in_=out_bank[:])
+        nc.sync.dma_start(out=out.rearrange("(r p) i -> p r i", p=P), in_=out_rows[:])

@@ -23,10 +23,15 @@ PASSES = O // K_PASS
 GROUPS = COLS // P
 FEATS = P // G
 ROW_TILES = B // P
-BLOCK_PASSES = 4
+BLOCK_PASSES = 2
 BASE_PASSES = COLS // I
 RUN = 4
-VECTOR_COLS = 576
+VECTOR_COLS = 512
+BASE_CHUNKS = PASSES // BASE_PASSES
+G_BUFS = 4
+FIRST_STEPS = 3
+RAW_BUFS = 4
+EARLY_SLOPES = 4
 
 FLOPS = 2 * B * O * (COLS + I)
 
@@ -40,6 +45,7 @@ def tile_advancedkanlayer_pa_k_kernel(
         keep = ctx.enter_context(tc.tile_pool(name="keep", bufs=1))
         stream = ctx.enter_context(tc.tile_pool(name="stream", bufs=2))
         psum = ctx.enter_context(tc.psum_pool(name="psum", bufs=1))
+        ctx.enter_context(tc.manual_schedule())
 
         def bank(n, shape, dtype, name):
             return psum.tile(shape, dtype, tag="bank%d" % n, name=name)
@@ -94,144 +100,178 @@ def tile_advancedkanlayer_pa_k_kernel(
         xT = const.tile([P, B], BF16)
         nc.vector.tensor_copy(out=xT[:], in_=xT_bank[:])
 
-        slope = keep.tile([P, GROUPS, B], F32)
-        dist = []
-        for n in range(GROUPS):
-            x_spread = bank(4 + n % 3, [P, B], F32, "x_spread")
-            nc.tensor.matmul(
-                out=x_spread[:], lhsT=spread[:, P * n : P * (n + 1)], rhs=xT[:], start=True, stop=True
-            )
-            d = keep.tile([P, B], F32, tag="dist", bufs=GROUPS, name="d")
-            nc.scalar.activation(out=d[:], in_=x_spread[:], func=ACT.Abs, bias=neg_knot[:], scale=1.0)
-            nc.scalar.activation(
-                out=slope[:, n, :], in_=x_spread[:], func=ACT.Sign, bias=neg_knot[:], scale=1.0
-            )
-            dist.append(d)
-
         g_codes = keep.tile([P, PASSES, B], U32, align_bytes=64)
         g_scales = keep.tile([P, PASSES, B], U8, align_bytes=64)
+        slope = keep.tile([P, GROUPS, B], F32)
+        dist = []
         block_cols = BLOCK_PASSES * K_PASS
-        for blk in range(PASSES // BLOCK_PASSES):
-            g_rows = stream.tile([P, ROW_TILES * block_cols], BF16, tag="g_rows", bufs=2)
+        blocks = PASSES // BLOCK_PASSES
+
+        def load_block(blk):
+            g_rows = stream.tile([P, ROW_TILES * block_cols], BF16, tag="g_rows", bufs=G_BUFS)
             nc.sync.dma_start(
                 out=g_rows[:].rearrange("p (r o) -> p r o", r=ROW_TILES),
                 in_=grad_out[:, block_cols * blk : block_cols * (blk + 1)].rearrange(
                     "(r p) o -> p r o", p=P
                 ),
             )
-            g_words = g_rows[:].bitcast(F32).rearrange("p (r w) -> p r w", r=ROW_TILES)
-            for c in range(BLOCK_PASSES * blk, BLOCK_PASSES * (blk + 1)):
-                first_word = (K_PASS // 2) * (c % BLOCK_PASSES)
-                g_grouped = stream.tile([P, B * PACK], BF16, tag="g_grouped", bufs=3, align_bytes=64)
-                g_grouped_words = g_grouped[:].bitcast(F32).rearrange("p (b u) -> p b u", u=2)
-                for half in range(2):
-                    flipped = bank((2 * c + half) % 4, [P, 2, B // 2], F32, "flipped")
-                    for u in range(2):
-                        for r in range(2):
-                            nc.tensor.transpose(
-                                out=flipped[:, u, P * r : P * (r + 1)],
-                                in_=g_words[
-                                    :, 2 * half + r, first_word + P * u : first_word + P * (u + 1)
-                                ],
-                                identity=ident_f32[:],
-                            )
-                    nc.scalar.copy(
-                        out=g_grouped_words[:, (B // 2) * half : (B // 2) * (half + 1), :],
-                        in_=flipped[:].rearrange("p u b -> p b u"),
-                    )
-                nc.vector.quantize_mx(
-                    out=g_codes[:, c, :].bitcast(E5M2_X4), scales=g_scales[:, c, :], in_=g_grouped[:]
-                )
+            return g_rows[:].bitcast(F32).rearrange("p (r w) -> p r w", r=ROW_TILES)
 
-        def regroup(raw):
-            grouped = stream.tile([P, COLS, PACK], BF16, tag="w_grouped", bufs=2, align_bytes=64)
-            src = raw[:].rearrange("p t (c i) -> p c t i", i=RUN)
-            dst = grouped[:].rearrange("p (c i) t -> p c t i", i=RUN)
-            cut = VECTOR_COLS // RUN
-            nc.vector.tensor_copy(out=dst[:, :cut], in_=src[:, :cut])
-            nc.scalar.copy(out=dst[:, cut:], in_=src[:, cut:])
-            return grouped
-
-        def quantise(grouped, codes, scales):
+        def quantise_pass(c, g_grouped):
             nc.vector.quantize_mx(
-                out=codes.bitcast(E4M3_X4),
-                scales=scales,
-                in_=grouped[:].rearrange("p w t -> p (w t)"),
+                out=g_codes[:, c, :].bitcast(E5M2_X4), scales=g_scales[:, c, :], in_=g_grouped[:]
             )
 
-        base_rows = base_activation.rearrange(
-            "(c u p e) i -> u e p c i", c=PASSES, u=2, p=P, e=2
-        )
-        base_bank = bank(7, [P, B], F32, "base_bank")
-        for chunk in range(PASSES // BASE_PASSES):
-            passes = range(BASE_PASSES * chunk, BASE_PASSES * (chunk + 1))
-            raw = stream.tile([P, PACK, COLS], BF16, tag="w_raw", bufs=4, name="base_raw")
-            for u in range(2):
-                for e in range(2):
-                    nc.sync.dma_start(
-                        out=raw[:, 2 * u + e, :].rearrange("p (c i) -> p c i", i=I),
-                        in_=base_rows[u, e][:, passes[0] : passes[0] + BASE_PASSES, :],
-                    )
-            b_codes = keep.tile([P, COLS], U32, tag="b_codes", bufs=2, align_bytes=64)
-            b_scales = keep.tile([P, COLS], U8, tag="b_scales", bufs=2, align_bytes=64)
-            quantise(regroup(raw), b_codes[:], b_scales[:])
-            for c in passes:
-                cols = slice(I * (c % BASE_PASSES), I * (c % BASE_PASSES + 1))
-                nc.tensor.matmul_mx(
-                    out=base_bank[:],
-                    lhsT=b_codes[:, cols].bitcast(E4M3_X4),
-                    lhsT_scale=b_scales[:, cols],
-                    rhs=g_codes[:, c, :].bitcast(E5M2_X4),
-                    rhs_scale=g_scales[:, c, :],
-                    start=(c == 0),
-                    stop=(c == PASSES - 1),
+        x_spread = []
+
+        def distance_or_sign(step):
+            n = step // 2
+            if step % 2 == 0:
+                x_spread.append(bank(4 + n % 3, [P, B], F32, "x_spread"))
+                nc.tensor.matmul(
+                    out=x_spread[n][:], lhsT=spread[:, P * n : P * (n + 1)], rhs=xT[:], start=True, stop=True
                 )
+                d = keep.tile([P, B], F32, tag="dist", bufs=GROUPS, name="d")
+                nc.scalar.activation(out=d[:], in_=x_spread[n][:], func=ACT.Abs, bias=neg_knot[:], scale=1.0)
+                dist.append(d)
+            else:
+                nc.scalar.activation(
+                    out=slope[:, n, :], in_=x_spread[n][:], func=ACT.Sign, bias=neg_knot[:], scale=1.0
+                )
+
+        g_words = [load_block(blk) for blk in range(G_BUFS)]
+        for step in range(FIRST_STEPS):
+            distance_or_sign(step)
+        g_grouped_before = None
+        for c in range(PASSES):
+            if FIRST_STEPS + c < 2 * GROUPS:
+                distance_or_sign(FIRST_STEPS + c)
+
+            words = g_words[c // BLOCK_PASSES]
+            first_word = (K_PASS // 2) * (c % BLOCK_PASSES)
+            g_grouped = stream.tile([P, B * PACK], BF16, tag="g_grouped", bufs=3, align_bytes=64)
+            g_grouped_words = g_grouped[:].bitcast(F32).rearrange("p (b u) -> p b u", u=2)
+            for half in range(2):
+                flipped = bank((2 * c + half) % 4, [P, 2, B // 2], F32, "flipped")
+                for u in range(2):
+                    for r in range(2):
+                        nc.tensor.transpose(
+                            out=flipped[:, u, P * r : P * (r + 1)],
+                            in_=words[:, 2 * half + r, first_word + P * u : first_word + P * (u + 1)],
+                            identity=ident_f32[:],
+                        )
+                copy_out = nc.scalar.copy if half == 0 else nc.vector.tensor_copy
+                copy_out(
+                    out=g_grouped_words[:, (B // 2) * half : (B // 2) * (half + 1), :],
+                    in_=flipped[:].rearrange("p u b -> p b u"),
+                )
+            if c % BLOCK_PASSES == BLOCK_PASSES - 1 and c // BLOCK_PASSES + G_BUFS < blocks:
+                g_words.append(load_block(c // BLOCK_PASSES + G_BUFS))
+            if c > 0:
+                quantise_pass(c - 1, g_grouped_before)
+            g_grouped_before = g_grouped
+        quantise_pass(PASSES - 1, g_grouped_before)
+
+        base_rows = base_activation.rearrange("(k p e) i -> p k (e i)", p=P, e=2)
+        w_rows = spline_weight.rearrange("(c u p e) i g -> c p u (e i g)", c=PASSES, u=2, p=P, e=2)
+        chunks = BASE_CHUNKS + PASSES
+
+        def load_chunk(j):
+            if j < BASE_CHUNKS:
+                raw = stream.tile([P, BASE_PASSES, PACK, I], BF16, tag="raw", bufs=RAW_BUFS, name="base_raw")
+                nc.sync.dma_start(
+                    out=raw[:].rearrange("p c (u e) i -> p (c u) (e i)", u=2),
+                    in_=base_rows[:, 2 * BASE_PASSES * j : 2 * BASE_PASSES * (j + 1), :],
+                )
+            else:
+                raw = stream.tile([P, PACK, COLS], BF16, tag="raw", bufs=RAW_BUFS, name="w_raw")
+                nc.sync.dma_start(
+                    out=raw[:].rearrange("p (u e) w -> p u (e w)", u=2), in_=w_rows[j - BASE_CHUNKS]
+                )
+            return raw
+
+        def regroup(j, raw):
+            grouped = stream.tile([P, COLS, PACK], BF16, tag="grouped", bufs=3, align_bytes=64)
+            if j < BASE_CHUNKS:
+                nc.vector.tensor_copy(
+                    out=grouped[:].rearrange("p (c k r) t -> p c k t r", c=BASE_PASSES, r=RUN),
+                    in_=raw[:].rearrange("p c t (k r) -> p c k t r", r=RUN),
+                )
+            else:
+                src = raw[:].rearrange("p t (k r) -> p k t r", r=RUN)
+                dst = grouped[:].rearrange("p (k r) t -> p k t r", r=RUN)
+                cut = VECTOR_COLS // RUN
+                nc.vector.tensor_copy(out=dst[:, :cut], in_=src[:, :cut])
+                nc.scalar.copy(out=dst[:, cut:], in_=src[:, cut:])
+            return grouped
+
+        def quantise_chunk(grouped):
+            codes = stream.tile([P, COLS], U32, tag="codes", bufs=4, align_bytes=64)
+            scales = stream.tile([P, COLS], U8, tag="scales", bufs=4, align_bytes=64)
+            nc.vector.quantize_mx(
+                out=codes[:].bitcast(E4M3_X4),
+                scales=scales[:],
+                in_=grouped[:].rearrange("p w t -> p (w t)"),
+            )
+            return codes, scales
+
+        def multiply(acc, codes, scales, cols, c):
+            nc.tensor.matmul_mx(
+                out=acc[:],
+                lhsT=codes[:, cols].bitcast(E4M3_X4),
+                lhsT_scale=scales[:, cols],
+                rhs=g_codes[:, c, :].bitcast(E5M2_X4),
+                rhs_scale=g_scales[:, c, :],
+                start=(c == 0),
+                stop=(c == PASSES - 1),
+            )
+
+        def slope_of_group(n):
+            inner = dist[n]
+            outer = keep.tile([P, B], F32, tag="outer", bufs=4)
+            nc.scalar.activation(out=outer[:], in_=inner[:], func=ACT.Relu, bias=1.0, scale=-1.0)
+            nc.scalar.activation(out=inner[:], in_=inner[:], func=ACT.Relu, bias=0.5, scale=-1.0)
+            nc.scalar.square(out=outer[:], in_=outer[:])
+            nc.scalar.square(out=inner[:], in_=inner[:])
+            nc.vector.scalar_tensor_tensor(
+                out=inner[:], in0=inner[:], scalar=4.0, in1=outer[:], op0=ALU.mult, op1=ALU.subtract
+            )
+            nc.vector.tensor_tensor(out=slope[:, n, :], in0=inner[:], in1=slope[:, n, :], op=ALU.mult)
+
+        raws = [load_chunk(j) for j in range(RAW_BUFS)]
+
+        base_bank = bank(7, [P, B], F32, "base_bank")
+        base_grouped = []
+        for j in range(BASE_CHUNKS):
+            base_grouped.append(regroup(j, raws[j]))
+            raws.append(load_chunk(j + RAW_BUFS))
+        for j in range(BASE_CHUNKS):
+            codes, scales = quantise_chunk(base_grouped[j])
+            for k in range(BASE_PASSES):
+                multiply(base_bank, codes, scales, slice(I * k, I * (k + 1)), BASE_PASSES * j + k)
+
+        for n in range(EARLY_SLOPES):
+            slope_of_group(n)
         base_part = keep.tile([P, B], F32)
         nc.scalar.mul(out=base_part[:], in_=base_bank[:], mul=0.1)
 
-        for n in range(GROUPS):
-            d = dist[n]
-            outer = keep.tile([P, B], F32, tag="outer", bufs=2)
-            nc.vector.tensor_scalar(
-                out=outer[:], in0=d[:], scalar1=1.0, scalar2=1.0, op0=ALU.min, op1=ALU.subtract
-            )
-            nc.vector.tensor_scalar(
-                out=d[:], in0=d[:], scalar1=0.5, scalar2=0.5, op0=ALU.min, op1=ALU.subtract
-            )
-            nc.scalar.square(out=outer[:], in_=outer[:])
-            nc.scalar.square(out=d[:], in_=d[:])
-            nc.vector.scalar_tensor_tensor(
-                out=d[:], in0=d[:], scalar=4.0, in1=outer[:], op0=ALU.mult, op1=ALU.subtract
-            )
-            nc.vector.tensor_tensor(out=slope[:, n, :], in0=d[:], in1=slope[:, n, :], op=ALU.mult)
-
-        w_rows = spline_weight.rearrange(
-            "(c u p e) i g -> c p u (e i g)", c=PASSES, u=2, p=P, e=2
-        )
         h = [bank(n, [P, B], F32, "h%d" % n) for n in range(GROUPS)]
-        for c in range(PASSES):
-            raw = stream.tile([P, PACK, COLS], BF16, tag="w_raw", bufs=4, name="w_raw")
-            nc.sync.dma_start(
-                out=raw[:].rearrange("p (u e) w -> p u (e w)", u=2), in_=w_rows[c]
-            )
-            w_codes = stream.tile([P, COLS], U32, tag="w_codes", bufs=4, align_bytes=64)
-            w_scales = stream.tile([P, COLS], U8, tag="w_scales", bufs=4, align_bytes=64)
-            quantise(regroup(raw), w_codes[:], w_scales[:])
+        grouped_next = regroup(BASE_CHUNKS, raws[BASE_CHUNKS])
+        for j in range(BASE_CHUNKS, chunks):
+            grouped = grouped_next
+            if j + RAW_BUFS < chunks:
+                raws.append(load_chunk(j + RAW_BUFS))
+            if j + 1 < chunks:
+                grouped_next = regroup(j + 1, raws[j + 1])
+            codes, scales = quantise_chunk(grouped)
             for n in range(GROUPS):
-                cols = slice(P * n, P * (n + 1))
-                nc.tensor.matmul_mx(
-                    out=h[n][:],
-                    lhsT=w_codes[:, cols].bitcast(E4M3_X4),
-                    lhsT_scale=w_scales[:, cols],
-                    rhs=g_codes[:, c, :].bitcast(E5M2_X4),
-                    rhs_scale=g_scales[:, c, :],
-                    start=(c == 0),
-                    stop=(c == PASSES - 1),
-                )
+                multiply(h[n], codes, scales, slice(P * n, P * (n + 1)), j - BASE_CHUNKS)
 
         spline_bank = None
         for n in range(GROUPS):
-            weighted = stream.tile([P, B], F32, tag="weighted", bufs=3)
+            if n >= EARLY_SLOPES:
+                slope_of_group(n)
+            weighted = stream.tile([P, B], F32, tag="weighted", bufs=4)
             nc.vector.scalar_tensor_tensor(
                 out=weighted[:], in0=h[n][:], scalar=6.0, in1=slope[:, n, :], op0=ALU.mult, op1=ALU.mult
             )

@@ -24,14 +24,22 @@ GROUPS = COLS // P
 FEATS = P // G
 ROW_TILES = B // P
 BLOCK_PASSES = 2
+BLOCKS = PASSES // BLOCK_PASSES
 BASE_PASSES = COLS // I
-RUN = 4
-VECTOR_COLS = 512
 BASE_CHUNKS = PASSES // BASE_PASSES
-G_BUFS = 4
-FIRST_STEPS = 3
-RAW_BUFS = 4
-EARLY_SLOPES = 4
+CHUNKS = BASE_CHUNKS + PASSES
+RUN = 4
+VECTOR_SHARE = 9
+PIECE = 1024
+SPLIT = 6
+WIDE = (3, 5)
+RAW_BUFS = 7
+FIRST_STEPS = 2
+FIRST_JOB = 2
+SLOPE_COLS = 12 * COLS
+EARLY_GROUPS = 6
+FIRST_BASE = 4
+JOBS_PER_CHUNK = 3
 
 FLOPS = 2 * B * O * (COLS + I)
 
@@ -50,34 +58,65 @@ def tile_advancedkanlayer_pa_k_kernel(
         def bank(n, shape, dtype, name):
             return psum.tile(shape, dtype, tag="bank%d" % n, name=name)
 
+        knots = const.tile([P, G], BF16)
+        nc.scalar.dma_start(out=knots[:], in_=grid_points.partition_broadcast(P))
+        spark = const.tile([P, 1], F32)
+        nc.vector.memset(spark[:], 0.0)
+        nc.scalar.activation(out=spark[:], in_=spark[:], func=ACT.Abs)
+
         x_rows = const.tile([P, ROW_TILES, I], BF16)
         nc.sync.dma_start(out=x_rows[:], in_=x_norm.rearrange("(r p) i -> p r i", p=P))
-        knots = const.tile([P, G], BF16)
-        nc.sync.dma_start(out=knots[:], in_=grid_points.partition_broadcast(P))
 
-        ident_f32 = const.tile([P, P], F32)
-        make_identity(nc, ident_f32[:])
+        base_rows_in = base_activation.rearrange("(k p e) i -> p k (e i)", p=P, e=2)
+        w_rows_in = spline_weight.rearrange("(c u p e) i g -> c p u (e i g)", c=PASSES, u=2, p=P, e=2)
+        block_cols = BLOCK_PASSES * K_PASS
+        needs = [(BLOCK_PASSES * k, 0, k) for k in range(BLOCKS)]
+        needs += [(FIRST_JOB + JOBS_PER_CHUNK * j, 1, j) for j in range(CHUNKS)]
+        needs.sort()
+        loaded = {}
+        waiting = list(needs)
+
+        def load_next():
+            if not waiting:
+                return
+            need, kind, k = waiting[0]
+            waiting.remove(waiting[0])
+            raw = stream.tile([P, PACK * COLS], BF16, tag="raw", bufs=RAW_BUFS, name="raw")
+            loaded[(kind, k)] = raw
+            if kind == 0:
+                dst = raw[:].rearrange("p (r o) -> p r o", r=ROW_TILES)
+                src = grad_out[:, block_cols * k : block_cols * (k + 1)].rearrange(
+                    "(r p) o -> p r o", p=P
+                )
+                pieces = BLOCK_PASSES if k == 0 else 1
+                width = block_cols // pieces
+                for s in range(pieces):
+                    nc.sync.dma_start(
+                        out=dst[:, :, width * s : width * (s + 1)], in_=src[:, :, width * s : width * (s + 1)]
+                    )
+            elif k < BASE_CHUNKS:
+                nc.sync.dma_start(
+                    out=raw[:].rearrange("p (k w) -> p k w", k=2 * BASE_PASSES),
+                    in_=base_rows_in[:, 2 * BASE_PASSES * k : 2 * BASE_PASSES * (k + 1), :],
+                )
+            else:
+                nc.sync.dma_start(
+                    out=raw[:].rearrange("p (u w) -> p u w", u=2), in_=w_rows_in[k - BASE_CHUNKS]
+                )
+
+        for n in range(RAW_BUFS):
+            load_next()
+
         ident_bf16 = const.tile([P, P], BF16)
         make_identity(nc, ident_bf16[:])
+        ident_f32 = const.tile([P, P], F32)
+        make_identity(nc, ident_f32[:])
 
         spread = const.tile([P, COLS], BF16)
         nc.vector.tensor_copy(
             out=spread[:].rearrange("p (i g) -> p i g", g=G),
             in_=ident_bf16[:].unsqueeze(2).to_broadcast([P, P, G]),
         )
-        same_feature = const.tile([P, FEATS], F32)
-        nc.vector.tensor_reduce(
-            out=same_feature[:],
-            in_=ident_f32[:].rearrange("p (j g) -> p j g", g=G),
-            axis=AXIS_X,
-            op=ALU.add,
-        )
-        gather = const.tile([P, GROUPS, I], F32)
-        nc.vector.memset(gather[:], 0.0)
-        for n in range(GROUPS):
-            nc.vector.tensor_copy(
-                out=gather[:, n, FEATS * n : FEATS * (n + 1)], in_=same_feature[:]
-            )
         same_knot = const.tile([P, G], F32)
         nc.vector.tensor_reduce(
             out=same_knot[:],
@@ -85,13 +124,6 @@ def tile_advancedkanlayer_pa_k_kernel(
             axis=AXIS_X,
             op=ALU.add,
         )
-        own_knot = const.tile([P, G], F32)
-        nc.vector.tensor_tensor(out=own_knot[:], in0=same_knot[:], in1=knots[:], op=ALU.mult)
-        knot = const.tile([P, 1], F32)
-        nc.vector.tensor_reduce(out=knot[:], in_=own_knot[:], axis=AXIS_X, op=ALU.add)
-        neg_knot = const.tile([P, 1], F32)
-        nc.vector.tensor_scalar_mul(out=neg_knot[:], in0=knot[:], scalar1=-1.0)
-
         xT_bank = bank(7, [P, B], BF16, "xT_bank")
         for r in range(ROW_TILES):
             nc.tensor.transpose(
@@ -99,29 +131,17 @@ def tile_advancedkanlayer_pa_k_kernel(
             )
         xT = const.tile([P, B], BF16)
         nc.vector.tensor_copy(out=xT[:], in_=xT_bank[:])
+        own_knot = const.tile([P, G], F32)
+        nc.vector.scalar_tensor_tensor(
+            out=own_knot[:], in0=same_knot[:], scalar=-1.0, in1=knots[:], op0=ALU.mult, op1=ALU.mult
+        )
+        neg_knot = const.tile([P, 1], F32)
+        nc.vector.tensor_reduce(out=neg_knot[:], in_=own_knot[:], axis=AXIS_X, op=ALU.add)
 
         g_codes = keep.tile([P, PASSES, B], U32, align_bytes=64)
         g_scales = keep.tile([P, PASSES, B], U8, align_bytes=64)
+        dist = keep.tile([P, GROUPS, B], F32)
         slope = keep.tile([P, GROUPS, B], F32)
-        dist = []
-        block_cols = BLOCK_PASSES * K_PASS
-        blocks = PASSES // BLOCK_PASSES
-
-        def load_block(blk):
-            g_rows = stream.tile([P, ROW_TILES * block_cols], BF16, tag="g_rows", bufs=G_BUFS)
-            nc.sync.dma_start(
-                out=g_rows[:].rearrange("p (r o) -> p r o", r=ROW_TILES),
-                in_=grad_out[:, block_cols * blk : block_cols * (blk + 1)].rearrange(
-                    "(r p) o -> p r o", p=P
-                ),
-            )
-            return g_rows[:].bitcast(F32).rearrange("p (r w) -> p r w", r=ROW_TILES)
-
-        def quantise_pass(c, g_grouped):
-            nc.vector.quantize_mx(
-                out=g_codes[:, c, :].bitcast(E5M2_X4), scales=g_scales[:, c, :], in_=g_grouped[:]
-            )
-
         x_spread = []
 
         def distance_or_sign(step):
@@ -131,23 +151,16 @@ def tile_advancedkanlayer_pa_k_kernel(
                 nc.tensor.matmul(
                     out=x_spread[n][:], lhsT=spread[:, P * n : P * (n + 1)], rhs=xT[:], start=True, stop=True
                 )
-                d = keep.tile([P, B], F32, tag="dist", bufs=GROUPS, name="d")
-                nc.scalar.activation(out=d[:], in_=x_spread[n][:], func=ACT.Abs, bias=neg_knot[:], scale=1.0)
-                dist.append(d)
+                nc.scalar.activation(
+                    out=dist[:, n, :], in_=x_spread[n][:], func=ACT.Abs, bias=neg_knot[:], scale=1.0
+                )
             else:
                 nc.scalar.activation(
                     out=slope[:, n, :], in_=x_spread[n][:], func=ACT.Sign, bias=neg_knot[:], scale=1.0
                 )
 
-        g_words = [load_block(blk) for blk in range(G_BUFS)]
-        for step in range(FIRST_STEPS):
-            distance_or_sign(step)
-        g_grouped_before = None
-        for c in range(PASSES):
-            if FIRST_STEPS + c < 2 * GROUPS:
-                distance_or_sign(FIRST_STEPS + c)
-
-            words = g_words[c // BLOCK_PASSES]
+        def flip_pass(c):
+            words = loaded[(0, c // BLOCK_PASSES)][:].bitcast(F32).rearrange("p (r w) -> p r w", r=ROW_TILES)
             first_word = (K_PASS // 2) * (c % BLOCK_PASSES)
             g_grouped = stream.tile([P, B * PACK], BF16, tag="g_grouped", bufs=3, align_bytes=64)
             g_grouped_words = g_grouped[:].bitcast(F32).rearrange("p (b u) -> p b u", u=2)
@@ -160,137 +173,246 @@ def tile_advancedkanlayer_pa_k_kernel(
                             in_=words[:, 2 * half + r, first_word + P * u : first_word + P * (u + 1)],
                             identity=ident_f32[:],
                         )
-                copy_out = nc.scalar.copy if half == 0 else nc.vector.tensor_copy
+                copy_out = nc.vector.tensor_copy if half == 1 and c < FIRST_JOB else nc.scalar.copy
                 copy_out(
                     out=g_grouped_words[:, (B // 2) * half : (B // 2) * (half + 1), :],
                     in_=flipped[:].rearrange("p u b -> p b u"),
                 )
-            if c % BLOCK_PASSES == BLOCK_PASSES - 1 and c // BLOCK_PASSES + G_BUFS < blocks:
-                g_words.append(load_block(c // BLOCK_PASSES + G_BUFS))
-            if c > 0:
-                quantise_pass(c - 1, g_grouped_before)
-            g_grouped_before = g_grouped
-        quantise_pass(PASSES - 1, g_grouped_before)
+            if c % BLOCK_PASSES == BLOCK_PASSES - 1:
+                load_next()
+            return g_grouped
 
-        base_rows = base_activation.rearrange("(k p e) i -> p k (e i)", p=P, e=2)
-        w_rows = spline_weight.rearrange("(c u p e) i g -> c p u (e i g)", c=PASSES, u=2, p=P, e=2)
-        chunks = BASE_CHUNKS + PASSES
-
-        def load_chunk(j):
-            if j < BASE_CHUNKS:
-                raw = stream.tile([P, BASE_PASSES, PACK, I], BF16, tag="raw", bufs=RAW_BUFS, name="base_raw")
-                nc.sync.dma_start(
-                    out=raw[:].rearrange("p c (u e) i -> p (c u) (e i)", u=2),
-                    in_=base_rows[:, 2 * BASE_PASSES * j : 2 * BASE_PASSES * (j + 1), :],
-                )
-            else:
-                raw = stream.tile([P, PACK, COLS], BF16, tag="raw", bufs=RAW_BUFS, name="w_raw")
-                nc.sync.dma_start(
-                    out=raw[:].rearrange("p (u e) w -> p u (e w)", u=2), in_=w_rows[j - BASE_CHUNKS]
-                )
-            return raw
-
-        def regroup(j, raw):
-            grouped = stream.tile([P, COLS, PACK], BF16, tag="grouped", bufs=3, align_bytes=64)
-            if j < BASE_CHUNKS:
-                nc.vector.tensor_copy(
-                    out=grouped[:].rearrange("p (c k r) t -> p c k t r", c=BASE_PASSES, r=RUN),
-                    in_=raw[:].rearrange("p c t (k r) -> p c k t r", r=RUN),
-                )
-            else:
-                src = raw[:].rearrange("p t (k r) -> p k t r", r=RUN)
-                dst = grouped[:].rearrange("p (k r) t -> p k t r", r=RUN)
-                cut = VECTOR_COLS // RUN
-                nc.vector.tensor_copy(out=dst[:, :cut], in_=src[:, :cut])
-                nc.scalar.copy(out=dst[:, cut:], in_=src[:, cut:])
-            return grouped
-
-        def quantise_chunk(grouped):
-            codes = stream.tile([P, COLS], U32, tag="codes", bufs=4, align_bytes=64)
-            scales = stream.tile([P, COLS], U8, tag="scales", bufs=4, align_bytes=64)
+        def quantise_pass(c, g_grouped):
             nc.vector.quantize_mx(
-                out=codes[:].bitcast(E4M3_X4),
-                scales=scales[:],
-                in_=grouped[:].rearrange("p w t -> p (w t)"),
+                out=g_codes[:, c, :].bitcast(E5M2_X4), scales=g_scales[:, c, :], in_=g_grouped[:]
             )
-            return codes, scales
 
-        def multiply(acc, codes, scales, cols, c):
+        grouped = {}
+        regrouped = {}
+
+        def regroup(unit, share, copy):
+            j, first, last = unit
+            if unit not in grouped:
+                grouped[unit] = stream.tile(
+                    [P, COLS, PACK], BF16, tag="grouped", bufs=3, align_bytes=64, name="grouped"
+                )
+            begin, end = share
+            if j < BASE_CHUNKS:
+                src = loaded[(1, j)][:].rearrange("p (c t k r) -> p c k t r", c=BASE_PASSES, t=PACK, r=RUN)
+                dst = grouped[unit][:].rearrange("p (c k r) t -> p c k t r", c=BASE_PASSES, r=RUN)
+                step = I
+            else:
+                src = loaded[(1, j)][:].rearrange("p (t k r) -> p k t r", t=PACK, r=RUN)
+                dst = grouped[unit][:].rearrange("p (k r) t -> p k t r", r=RUN)
+                step = RUN
+            copy(
+                out=dst[:, begin // step : end // step],
+                in_=src[:, (first + begin) // step : (first + end) // step],
+            )
+            regrouped[j] = regrouped.get(j, 0) + end - begin
+            if regrouped[j] == COLS:
+                load_next()
+
+        codes = {}
+
+        def quantise_unit(unit):
+            j, first, last = unit
+            width = last - first
+            words = stream.tile([P, COLS], U32, tag="codes", bufs=6, align_bytes=64, name="words")
+            scales = stream.tile([P, COLS], U8, tag="scales", bufs=6, align_bytes=64, name="scales")
+            begin = 0
+            while begin < width:
+                end = begin + PIECE
+                while end > width:
+                    end = begin + (end - begin) // 2
+                nc.vector.quantize_mx(
+                    out=words[:, begin:end].bitcast(E4M3_X4),
+                    scales=scales[:, begin:end],
+                    in_=grouped[unit][:].rearrange("p w t -> p (w t)")[:, PACK * begin : PACK * end],
+                )
+                begin = end
+            codes[unit] = (words, scales)
+
+        def multiply(acc, unit, column, c):
+            words, scales = codes[unit]
             nc.tensor.matmul_mx(
                 out=acc[:],
-                lhsT=codes[:, cols].bitcast(E4M3_X4),
-                lhsT_scale=scales[:, cols],
+                lhsT=words[:, column : column + P].bitcast(E4M3_X4),
+                lhsT_scale=scales[:, column : column + P],
                 rhs=g_codes[:, c, :].bitcast(E5M2_X4),
                 rhs_scale=g_scales[:, c, :],
                 start=(c == 0),
                 stop=(c == PASSES - 1),
             )
 
-        def slope_of_group(n):
-            inner = dist[n]
-            outer = keep.tile([P, B], F32, tag="outer", bufs=4)
-            nc.scalar.activation(out=outer[:], in_=inner[:], func=ACT.Relu, bias=1.0, scale=-1.0)
-            nc.scalar.activation(out=inner[:], in_=inner[:], func=ACT.Relu, bias=0.5, scale=-1.0)
-            nc.scalar.square(out=outer[:], in_=outer[:])
-            nc.scalar.square(out=inner[:], in_=inner[:])
-            nc.vector.scalar_tensor_tensor(
-                out=inner[:], in0=inner[:], scalar=4.0, in1=outer[:], op0=ALU.mult, op1=ALU.subtract
+        scalar_steps = []
+        vector_steps = []
+        for n in range(0, GROUPS, 2):
+            outer = keep.tile([P, 2, B], F32, tag="outer", bufs=2, name="outer")
+            inner = dist[:, n : n + 2, :]
+            sign = slope[:, n : n + 2, :]
+            scalar_steps.append(
+                lambda o=outer, i=inner: nc.scalar.activation(out=o[:], in_=i, func=ACT.Relu, bias=1.0, scale=-1.0)
             )
-            nc.vector.tensor_tensor(out=slope[:, n, :], in0=inner[:], in1=slope[:, n, :], op=ALU.mult)
+            scalar_steps.append(
+                lambda i=inner: nc.scalar.activation(out=i, in_=i, func=ACT.Relu, bias=0.5, scale=-1.0)
+            )
+            scalar_steps.append(lambda o=outer: nc.scalar.square(out=o[:], in_=o[:]))
+            scalar_steps.append(lambda i=inner: nc.scalar.square(out=i, in_=i))
+            vector_steps.append(
+                lambda o=outer, i=inner: nc.vector.scalar_tensor_tensor(
+                    out=i, in0=i, scalar=4.0, in1=o[:], op0=ALU.mult, op1=ALU.subtract
+                )
+            )
+            vector_steps.append(
+                lambda i=inner, s=sign: nc.vector.tensor_tensor(out=s, in0=i, in1=s, op=ALU.mult)
+            )
 
-        raws = [load_chunk(j) for j in range(RAW_BUFS)]
+        done = {"scalar": 0, "vector": 0}
+
+        def slope_steps(goal):
+            while done["vector"] < 2 * (done["scalar"] // 4):
+                vector_steps[done["vector"]]()
+                done["vector"] += 1
+            while done["scalar"] < min(goal, len(scalar_steps)):
+                scalar_steps[done["scalar"]]()
+                done["scalar"] += 1
+
+        early_cols = P * EARLY_GROUPS
+        split = range(CHUNKS - SPLIT, CHUNKS)
+        units = [(j, 0, COLS) for j in range(CHUNKS - SPLIT)]
+        units += [(j, 0, early_cols) for j in split]
+        units += [(j, early_cols, COLS) for j in split]
+        jobs = []
+        for unit in units:
+            jobs.append(lambda u=unit: regroup(u, (0, COLS // 2), nc.vector.tensor_copy))
+            jobs.append(lambda u=unit: regroup(u, (COLS // 2, COLS), nc.vector.tensor_copy))
+            jobs.append(lambda u=unit: quantise_unit(u))
 
         base_bank = bank(7, [P, B], F32, "base_bank")
-        base_grouped = []
-        for j in range(BASE_CHUNKS):
-            base_grouped.append(regroup(j, raws[j]))
-            raws.append(load_chunk(j + RAW_BUFS))
-        for j in range(BASE_CHUNKS):
-            codes, scales = quantise_chunk(base_grouped[j])
-            for k in range(BASE_PASSES):
-                multiply(base_bank, codes, scales, slice(I * k, I * (k + 1)), BASE_PASSES * j + k)
 
-        for n in range(EARLY_SLOPES):
-            slope_of_group(n)
-        base_part = keep.tile([P, B], F32)
-        nc.scalar.mul(out=base_part[:], in_=base_bank[:], mul=0.1)
+        def multiply_base(c):
+            multiply(base_bank, units[c // BASE_PASSES], I * (c % BASE_PASSES), c)
 
-        h = [bank(n, [P, B], F32, "h%d" % n) for n in range(GROUPS)]
-        grouped_next = regroup(BASE_CHUNKS, raws[BASE_CHUNKS])
-        for j in range(BASE_CHUNKS, chunks):
-            grouped = grouped_next
-            if j + RAW_BUFS < chunks:
-                raws.append(load_chunk(j + RAW_BUFS))
-            if j + 1 < chunks:
-                grouped_next = regroup(j + 1, raws[j + 1])
-            codes, scales = quantise_chunk(grouped)
-            for n in range(GROUPS):
-                multiply(h[n], codes, scales, slice(P * n, P * (n + 1)), j - BASE_CHUNKS)
+        for step in range(FIRST_STEPS):
+            distance_or_sign(step)
+        g_grouped_before = None
+        for c in range(PASSES):
+            g_grouped = flip_pass(c)
+            if FIRST_STEPS + c < 2 * GROUPS:
+                distance_or_sign(FIRST_STEPS + c)
+            if c >= FIRST_JOB:
+                jobs[c - FIRST_JOB]()
+            if c > 0:
+                quantise_pass(c - 1, g_grouped_before)
+            if c in WIDE:
+                slope_steps(done["scalar"] + 1)
+            g_grouped_before = g_grouped
+            if c >= FIRST_BASE:
+                multiply_base(c - FIRST_BASE)
+        quantise_pass(PASSES - 1, g_grouped_before)
+        ready = (PASSES - FIRST_JOB) // JOBS_PER_CHUNK
 
-        spline_bank = None
-        for n in range(GROUPS):
-            if n >= EARLY_SLOPES:
-                slope_of_group(n)
-            weighted = stream.tile([P, B], F32, tag="weighted", bufs=4)
+        for c in range(PASSES - FIRST_BASE, PASSES):
+            multiply_base(c)
+        h = [bank(n, [P, B], F32, "h%d" % n) for n in range(GROUPS - 1)]
+
+        def multiply_unit(unit, groups):
+            j, first, last = unit
+            for n in groups:
+                if first <= P * n < last:
+                    multiply(h[n], unit, P * n - first, j - BASE_CHUNKS)
+
+        weighted = {}
+        flat = {}
+        spline_rows = keep.tile([P, ROW_TILES, I], F32)
+
+        def weigh(n):
+            weighted[n] = stream.tile([P, B], F32, tag="weighted", bufs=4, name="weighted")
             nc.vector.scalar_tensor_tensor(
-                out=weighted[:], in0=h[n][:], scalar=6.0, in1=slope[:, n, :], op0=ALU.mult, op1=ALU.mult
+                out=weighted[n][:], in0=h[n][:], scalar=6.0, in1=slope[:, n, :], op0=ALU.mult, op1=ALU.mult
             )
-            if n == 0:
-                spline_bank = bank(0, [P, B], F32, "spline_bank")
-            nc.tensor.matmul(
-                out=spline_bank[:],
-                lhsT=gather[:, n, :],
-                rhs=weighted[:],
-                start=(n == 0),
-                stop=(n == GROUPS - 1),
+
+        def flip_group(n):
+            flat[n] = bank(n, [P, ROW_TILES, P], F32, "flat")
+            for r in range(ROW_TILES):
+                nc.tensor.transpose(
+                    out=flat[n][:, r, :], in_=weighted[n][:, P * r : P * (r + 1)], identity=ident_f32[:]
+                )
+
+        def add_neighbours(n):
+            nc.vector.tensor_reduce(
+                out=spline_rows[:, :, FEATS * n : FEATS * (n + 1)],
+                in_=flat[n][:].rearrange("p r (j g) -> p r j g", g=G),
+                axis=AXIS_X,
+                op=ALU.add,
             )
-        outT = keep.tile([P, B], F32)
-        nc.vector.tensor_tensor(out=outT[:], in0=spline_bank[:], in1=base_part[:], op=ALU.add)
-        out_bank = bank(1, [P, ROW_TILES, I], F32, "out_bank")
-        for r in range(ROW_TILES):
-            nc.tensor.transpose(
-                out=out_bank[:, r, :], in_=outT[:, P * r : P * (r + 1)], identity=ident_f32[:]
-            )
+
+        def close_group(n):
+            weigh(n)
+            flip_group(n)
+
         out_rows = keep.tile([P, ROW_TILES, I], F32)
-        nc.vector.tensor_copy(out=out_rows[:], in_=out_bank[:])
-        nc.sync.dma_start(out=out.rearrange("(r p) i -> p r i", p=P), in_=out_rows[:])
+
+        def store(groups):
+            cols = slice(FEATS * groups[0], FEATS * (groups[-1] + 1))
+            nc.vector.tensor_tensor(
+                out=out_rows[:, :, cols], in0=spline_rows[:, :, cols], in1=base_rows[:, :, cols], op=ALU.add
+            )
+            nc.sync.dma_start(
+                out=out.rearrange("(r p) i -> p r i", p=P)[:, :, cols], in_=out_rows[:, :, cols]
+            )
+
+        early = range(EARLY_GROUPS)
+        late = range(EARLY_GROUPS, GROUPS)
+        early_steps = []
+        for n in early:
+            early_steps.append(lambda n=n: close_group(n))
+            if n > 0:
+                early_steps.append(lambda n=n: add_neighbours(n - 1))
+        early_steps.append(lambda: add_neighbours(EARLY_GROUPS - 1))
+
+        base_part = keep.tile([P, B], F32)
+        base_rows = keep.tile([P, ROW_TILES, I], F32)
+        regroup_next = -(-(PASSES - FIRST_JOB) // JOBS_PER_CHUNK)
+        columns = 0
+        first_goal = done["scalar"]
+        for k in range(ready, len(units)):
+            while regroup_next < len(units) and regroup_next <= k + 1:
+                unit = units[regroup_next]
+                width = unit[2] - unit[1]
+                cut = width * VECTOR_SHARE // 16 if unit not in units[-SPLIT:] else 0
+                if cut > 0:
+                    regroup(unit, (0, cut), nc.vector.tensor_copy)
+                regroup(unit, (cut, width), nc.scalar.copy)
+                regroup_next += 1
+            unit = units[k]
+            quantise_unit(unit)
+            columns += unit[2] - unit[1]
+            slope_steps(first_goal + (len(scalar_steps) - first_goal) * columns // SLOPE_COLS)
+            if k == ready:
+                nc.scalar.mul(out=base_part[:], in_=base_bank[:], mul=0.1)
+                base_flipped = bank(7, [P, ROW_TILES, I], F32, "base_flipped")
+                for r in range(ROW_TILES):
+                    nc.tensor.transpose(
+                        out=base_flipped[:, r, :], in_=base_part[:, P * r : P * (r + 1)], identity=ident_f32[:]
+                    )
+                nc.scalar.copy(out=base_rows[:], in_=base_flipped[:])
+                for u in units[BASE_CHUNKS:ready]:
+                    multiply_unit(u, range(GROUPS - 1))
+                h.append(bank(7, [P, B], F32, "h7"))
+                for u in units[BASE_CHUNKS:ready]:
+                    multiply_unit(u, range(GROUPS - 1, GROUPS))
+            multiply_unit(unit, range(GROUPS))
+            if unit in units[-SPLIT:]:
+                s = units[-SPLIT:].index(unit)
+                share = range(len(early_steps) * s // SPLIT, len(early_steps) * (s + 1) // SPLIT)
+                for e in share:
+                    early_steps[e]()
+
+        for n in late:
+            close_group(n)
+        store(early)
+        for n in late:
+            add_neighbours(n)
+        store(late)

@@ -29,16 +29,19 @@ BASE_PASSES = COLS // I
 BASE_CHUNKS = PASSES // BASE_PASSES
 CHUNKS = BASE_CHUNKS + PASSES
 RUN = 4
-VECTOR_SHARE = 9
+EARLY_STEPS = 12
+VECTOR_SHARE = 17
 PIECE = 1024
 SPLIT = 6
-WIDE = (3, 5)
+WIDE = (3,5,7,9,11,13)
 RAW_BUFS = 7
 FIRST_STEPS = 2
 FIRST_JOB = 2
 SLOPE_COLS = 12 * COLS
 EARLY_GROUPS = 6
-FIRST_BASE = 4
+BASE_RATE = 2
+BASE_AFTER = 2
+HELP = 2
 JOBS_PER_CHUNK = 3
 
 FLOPS = 2 * B * O * (COLS + I)
@@ -67,11 +70,14 @@ def tile_advancedkanlayer_pa_k_kernel(
         x_rows = const.tile([P, ROW_TILES, I], BF16)
         nc.sync.dma_start(out=x_rows[:], in_=x_norm.rearrange("(r p) i -> p r i", p=P))
 
-        base_rows_in = base_activation.rearrange("(k p e) i -> p k (e i)", p=P, e=2)
-        w_rows_in = spline_weight.rearrange("(c u p e) i g -> c p u (e i g)", c=PASSES, u=2, p=P, e=2)
+        base_rows_in = base_activation.rearrange("(c p t) i -> p c (t i)", p=P, t=PACK)
+        w_rows_in = spline_weight.rearrange("(c p t) i g -> c p (t i g)", p=P, t=PACK)
         block_cols = BLOCK_PASSES * K_PASS
         needs = [(BLOCK_PASSES * k, 0, k) for k in range(BLOCKS)]
-        needs += [(FIRST_JOB + JOBS_PER_CHUNK * j, 1, j) for j in range(CHUNKS)]
+        base_chunks = list(range(BASE_CHUNKS))
+        spline_chunks = list(range(BASE_CHUNKS, CHUNKS))
+        order = spline_chunks[:BASE_AFTER] + base_chunks + spline_chunks[BASE_AFTER:]
+        needs += [(FIRST_JOB + JOBS_PER_CHUNK * s, 1, order[s]) for s in range(CHUNKS)]
         needs.sort()
         loaded = {}
         waiting = list(needs)
@@ -96,13 +102,11 @@ def tile_advancedkanlayer_pa_k_kernel(
                     )
             elif k < BASE_CHUNKS:
                 nc.sync.dma_start(
-                    out=raw[:].rearrange("p (k w) -> p k w", k=2 * BASE_PASSES),
-                    in_=base_rows_in[:, 2 * BASE_PASSES * k : 2 * BASE_PASSES * (k + 1), :],
+                    out=raw[:].rearrange("p (c w) -> p c w", c=BASE_PASSES),
+                    in_=base_rows_in[:, BASE_PASSES * k : BASE_PASSES * (k + 1), :],
                 )
             else:
-                nc.sync.dma_start(
-                    out=raw[:].rearrange("p (u w) -> p u w", u=2), in_=w_rows_in[k - BASE_CHUNKS]
-                )
+                nc.sync.dma_start(out=raw[:], in_=w_rows_in[k - BASE_CHUNKS])
 
         for n in range(RAW_BUFS):
             load_next()
@@ -170,10 +174,10 @@ def tile_advancedkanlayer_pa_k_kernel(
                     for r in range(2):
                         nc.tensor.transpose(
                             out=flipped[:, u, P * r : P * (r + 1)],
-                            in_=words[:, 2 * half + r, first_word + P * u : first_word + P * (u + 1)],
+                            in_=words[:, 2 * half + r, first_word + u : first_word + 2 * P : 2],
                             identity=ident_f32[:],
                         )
-                copy_out = nc.vector.tensor_copy if half == 1 and c < FIRST_JOB else nc.scalar.copy
+                copy_out = nc.vector.tensor_copy if half == 1 and c < HELP else nc.scalar.copy
                 copy_out(
                     out=g_grouped_words[:, (B // 2) * half : (B // 2) * (half + 1), :],
                     in_=flipped[:].rearrange("p u b -> p b u"),
@@ -271,7 +275,7 @@ def tile_advancedkanlayer_pa_k_kernel(
         done = {"scalar": 0, "vector": 0}
 
         def slope_steps(goal):
-            while done["vector"] < 2 * (done["scalar"] // 4):
+            if done["vector"] < 2 * (done["scalar"] // 4):
                 vector_steps[done["vector"]]()
                 done["vector"] += 1
             while done["scalar"] < min(goal, len(scalar_steps)):
@@ -279,8 +283,8 @@ def tile_advancedkanlayer_pa_k_kernel(
                 done["scalar"] += 1
 
         early_cols = P * EARLY_GROUPS
-        split = range(CHUNKS - SPLIT, CHUNKS)
-        units = [(j, 0, COLS) for j in range(CHUNKS - SPLIT)]
+        split = order[-SPLIT:]
+        units = [(j, 0, COLS) for j in order[:-SPLIT]]
         units += [(j, 0, early_cols) for j in split]
         units += [(j, early_cols, COLS) for j in split]
         jobs = []
@@ -291,8 +295,14 @@ def tile_advancedkanlayer_pa_k_kernel(
 
         base_bank = bank(7, [P, B], F32, "base_bank")
 
-        def multiply_base(c):
-            multiply(base_bank, units[c // BASE_PASSES], I * (c % BASE_PASSES), c)
+        base_next = [0]
+
+        def multiply_base(most):
+            c = base_next[0]
+            while c < most and (c // BASE_PASSES, 0, COLS) in codes:
+                multiply(base_bank, (c // BASE_PASSES, 0, COLS), I * (c % BASE_PASSES), c)
+                c += 1
+            base_next[0] = c
 
         for step in range(FIRST_STEPS):
             distance_or_sign(step)
@@ -308,13 +318,13 @@ def tile_advancedkanlayer_pa_k_kernel(
             if c in WIDE:
                 slope_steps(done["scalar"] + 1)
             g_grouped_before = g_grouped
-            if c >= FIRST_BASE:
-                multiply_base(c - FIRST_BASE)
+            multiply_base(min(base_next[0] + BASE_RATE, c - 1))
         quantise_pass(PASSES - 1, g_grouped_before)
+        if (PASSES - FIRST_JOB) % JOBS_PER_CHUNK == 1:
+            jobs[PASSES - FIRST_JOB]()
         ready = (PASSES - FIRST_JOB) // JOBS_PER_CHUNK
 
-        for c in range(PASSES - FIRST_BASE, PASSES):
-            multiply_base(c)
+        multiply_base(PASSES)
         h = [bank(n, [P, B], F32, "h%d" % n) for n in range(GROUPS - 1)]
 
         def multiply_unit(unit, groups):
@@ -381,7 +391,7 @@ def tile_advancedkanlayer_pa_k_kernel(
             while regroup_next < len(units) and regroup_next <= k + 1:
                 unit = units[regroup_next]
                 width = unit[2] - unit[1]
-                cut = width * VECTOR_SHARE // 16 if unit not in units[-SPLIT:] else 0
+                cut = width * VECTOR_SHARE // 32 // RUN // 2 * RUN * 2 if unit not in units[-SPLIT:] else 0
                 if cut > 0:
                     regroup(unit, (0, cut), nc.vector.tensor_copy)
                 regroup(unit, (cut, width), nc.scalar.copy)
@@ -389,7 +399,10 @@ def tile_advancedkanlayer_pa_k_kernel(
             unit = units[k]
             quantise_unit(unit)
             columns += unit[2] - unit[1]
-            slope_steps(first_goal + (len(scalar_steps) - first_goal) * columns // SLOPE_COLS)
+            if unit in units[-SPLIT:]:
+                slope_steps(done["scalar"] + 1)
+            else:
+                slope_steps(first_goal + (EARLY_STEPS - first_goal) * columns // SLOPE_COLS)
             if k == ready:
                 nc.scalar.mul(out=base_part[:], in_=base_bank[:], mul=0.1)
                 base_flipped = bank(7, [P, ROW_TILES, I], F32, "base_flipped")
@@ -398,10 +411,11 @@ def tile_advancedkanlayer_pa_k_kernel(
                         out=base_flipped[:, r, :], in_=base_part[:, P * r : P * (r + 1)], identity=ident_f32[:]
                     )
                 nc.scalar.copy(out=base_rows[:], in_=base_flipped[:])
-                for u in units[BASE_CHUNKS:ready]:
+                before = [u for u in units[:ready] if u[0] >= BASE_CHUNKS]
+                for u in before:
                     multiply_unit(u, range(GROUPS - 1))
                 h.append(bank(7, [P, B], F32, "h7"))
-                for u in units[BASE_CHUNKS:ready]:
+                for u in before:
                     multiply_unit(u, range(GROUPS - 1, GROUPS))
             multiply_unit(unit, range(GROUPS))
             if unit in units[-SPLIT:]:
@@ -410,6 +424,8 @@ def tile_advancedkanlayer_pa_k_kernel(
                 for e in share:
                     early_steps[e]()
 
+        while done["vector"] < len(vector_steps):
+            slope_steps(len(scalar_steps))
         for n in late:
             close_group(n)
         store(early)

@@ -29,18 +29,21 @@ BASE_PASSES = COLS // I
 BASE_CHUNKS = PASSES // BASE_PASSES
 CHUNKS = BASE_CHUNKS + PASSES
 RUN = 4
-EARLY_STEPS = 12
-VECTOR_SHARE = 17
+EARLY_STEPS = 9
+VECTOR_SHARE = 16
 PIECE = 1024
-SPLIT = 6
-WIDE = (3,5,7,9,11,13)
-RAW_BUFS = 7
+SPLIT = 7
+WIDE = (3,5,7,9,11)
+RAW_BUFS = 8
 FIRST_STEPS = 2
-FIRST_JOB = 2
-SLOPE_COLS = 12 * COLS
+FIRST_JOB = 3
+SLOPE_COLS = 11 * COLS
 EARLY_GROUPS = 6
 BASE_RATE = 2
 BASE_AFTER = 2
+WEIGHTED_BUFS = 2
+G_BUFS = 2
+LATE_RATE = 1
 HELP = 2
 JOBS_PER_CHUNK = 3
 
@@ -66,6 +69,8 @@ def tile_advancedkanlayer_pa_k_kernel(
         spark = const.tile([P, 1], F32)
         nc.vector.memset(spark[:], 0.0)
         nc.scalar.activation(out=spark[:], in_=spark[:], func=ACT.Abs)
+        minus_one = const.tile([P, 1], F32)
+        nc.vector.memset(minus_one[:], -1.0)
 
         x_rows = const.tile([P, ROW_TILES, I], BF16)
         nc.sync.dma_start(out=x_rows[:], in_=x_norm.rearrange("(r p) i -> p r i", p=P))
@@ -141,6 +146,8 @@ def tile_advancedkanlayer_pa_k_kernel(
         )
         neg_knot = const.tile([P, 1], F32)
         nc.vector.tensor_reduce(out=neg_knot[:], in_=own_knot[:], axis=AXIS_X, op=ALU.add)
+        half_knot = const.tile([P, 1], F32)
+        nc.vector.tensor_scalar(out=half_knot[:], in0=neg_knot[:], scalar1=0.5, scalar2=None, op0=ALU.add)
 
         g_codes = keep.tile([P, PASSES, B], U32, align_bytes=64)
         g_scales = keep.tile([P, PASSES, B], U8, align_bytes=64)
@@ -148,7 +155,7 @@ def tile_advancedkanlayer_pa_k_kernel(
         slope = keep.tile([P, GROUPS, B], F32)
         x_spread = []
 
-        def distance_or_sign(step):
+        def distance(step):
             n = step // 2
             if step % 2 == 0:
                 x_spread.append(bank(4 + n % 3, [P, B], F32, "x_spread"))
@@ -160,13 +167,13 @@ def tile_advancedkanlayer_pa_k_kernel(
                 )
             else:
                 nc.scalar.activation(
-                    out=slope[:, n, :], in_=x_spread[n][:], func=ACT.Sign, bias=neg_knot[:], scale=1.0
+                    out=slope[:, n, :], in_=x_spread[n][:], func=ACT.Abs, bias=half_knot[:], scale=1.0
                 )
 
         def flip_pass(c):
             words = loaded[(0, c // BLOCK_PASSES)][:].bitcast(F32).rearrange("p (r w) -> p r w", r=ROW_TILES)
             first_word = (K_PASS // 2) * (c % BLOCK_PASSES)
-            g_grouped = stream.tile([P, B * PACK], BF16, tag="g_grouped", bufs=3, align_bytes=64)
+            g_grouped = stream.tile([P, B * PACK], BF16, tag="g_grouped", bufs=G_BUFS, align_bytes=64)
             g_grouped_words = g_grouped[:].bitcast(F32).rearrange("p (b u) -> p b u", u=2)
             for half in range(2):
                 flipped = bank((2 * c + half) % 4, [P, 2, B // 2], F32, "flipped")
@@ -252,30 +259,31 @@ def tile_advancedkanlayer_pa_k_kernel(
         scalar_steps = []
         vector_steps = []
         for n in range(0, GROUPS, 2):
-            outer = keep.tile([P, 2, B], F32, tag="outer", bufs=2, name="outer")
-            inner = dist[:, n : n + 2, :]
-            sign = slope[:, n : n + 2, :]
+            inner = keep.tile([P, 2, B], F32, tag="inner", bufs=2, name="inner")
+            outer = dist[:, n : n + 2, :]
+            zigzag = slope[:, n : n + 2, :]
             scalar_steps.append(
-                lambda o=outer, i=inner: nc.scalar.activation(out=o[:], in_=i, func=ACT.Relu, bias=1.0, scale=-1.0)
+                lambda o=inner, i=outer: nc.scalar.activation(out=o[:], in_=i, func=ACT.Relu, bias=1.0, scale=-2.0)
             )
             scalar_steps.append(
-                lambda i=inner: nc.scalar.activation(out=i, in_=i, func=ACT.Relu, bias=0.5, scale=-1.0)
+                lambda i=outer: nc.scalar.activation(out=i, in_=i, func=ACT.Relu, bias=1.0, scale=-1.0)
             )
-            scalar_steps.append(lambda o=outer: nc.scalar.square(out=o[:], in_=o[:]))
-            scalar_steps.append(lambda i=inner: nc.scalar.square(out=i, in_=i))
+            scalar_steps.append(
+                lambda z=zigzag: nc.scalar.activation(out=z, in_=z, func=ACT.Abs, bias=minus_one[:], scale=1.0)
+            )
             vector_steps.append(
-                lambda o=outer, i=inner: nc.vector.scalar_tensor_tensor(
-                    out=i, in0=i, scalar=4.0, in1=o[:], op0=ALU.mult, op1=ALU.subtract
+                lambda o=inner, i=outer: nc.vector.tensor_tensor(out=o[:], in0=o[:], in1=i, op=ALU.add)
+            )
+            vector_steps.append(
+                lambda o=inner, z=zigzag: nc.vector.scalar_tensor_tensor(
+                    out=z, in0=z, scalar=0.5, in1=o[:], op0=ALU.subtract, op1=ALU.mult
                 )
-            )
-            vector_steps.append(
-                lambda i=inner, s=sign: nc.vector.tensor_tensor(out=s, in0=i, in1=s, op=ALU.mult)
             )
 
         done = {"scalar": 0, "vector": 0}
 
         def slope_steps(goal):
-            if done["vector"] < 2 * (done["scalar"] // 4):
+            if done["vector"] < 2 * (done["scalar"] // 3):
                 vector_steps[done["vector"]]()
                 done["vector"] += 1
             while done["scalar"] < min(goal, len(scalar_steps)):
@@ -305,12 +313,12 @@ def tile_advancedkanlayer_pa_k_kernel(
             base_next[0] = c
 
         for step in range(FIRST_STEPS):
-            distance_or_sign(step)
+            distance(step)
         g_grouped_before = None
         for c in range(PASSES):
             g_grouped = flip_pass(c)
             if FIRST_STEPS + c < 2 * GROUPS:
-                distance_or_sign(FIRST_STEPS + c)
+                distance(FIRST_STEPS + c)
             if c >= FIRST_JOB:
                 jobs[c - FIRST_JOB]()
             if c > 0:
@@ -338,7 +346,8 @@ def tile_advancedkanlayer_pa_k_kernel(
         spline_rows = keep.tile([P, ROW_TILES, I], F32)
 
         def weigh(n):
-            weighted[n] = stream.tile([P, B], F32, tag="weighted", bufs=4, name="weighted")
+            assert done["vector"] >= 2 * (n // 2 + 1)
+            weighted[n] = stream.tile([P, B], F32, tag="weighted", bufs=WEIGHTED_BUFS, name="weighted")
             nc.vector.scalar_tensor_tensor(
                 out=weighted[n][:], in0=h[n][:], scalar=6.0, in1=slope[:, n, :], op0=ALU.mult, op1=ALU.mult
             )
@@ -400,7 +409,7 @@ def tile_advancedkanlayer_pa_k_kernel(
             quantise_unit(unit)
             columns += unit[2] - unit[1]
             if unit in units[-SPLIT:]:
-                slope_steps(done["scalar"] + 1)
+                slope_steps(done["scalar"] + LATE_RATE)
             else:
                 slope_steps(first_goal + (EARLY_STEPS - first_goal) * columns // SLOPE_COLS)
             if k == ready:

@@ -29,21 +29,21 @@ BASE_PASSES = COLS // I
 BASE_CHUNKS = PASSES // BASE_PASSES
 CHUNKS = BASE_CHUNKS + PASSES
 RUN = 4
-EARLY_STEPS = 9
-VECTOR_SHARE = 16
+LATE_SHARE = 14
+VECTOR_SHARE = 10
 PIECE = 1024
-SPLIT = 7
-WIDE = (3,5,7,9,11)
+SPLIT = 8
+WIDE = (5, 7, 9, 13)
+V_SLOPE = (0, 0, 0, 1, 1, 0, 0, 1, 1, 0, 0, 1, 1, 0, 0, 1)
+V_RATE = 1
 RAW_BUFS = 8
 FIRST_STEPS = 2
 FIRST_JOB = 3
-SLOPE_COLS = 11 * COLS
 EARLY_GROUPS = 6
 BASE_RATE = 2
 BASE_AFTER = 2
 WEIGHTED_BUFS = 2
 G_BUFS = 2
-LATE_RATE = 1
 HELP = 2
 JOBS_PER_CHUNK = 3
 
@@ -157,6 +157,7 @@ def tile_advancedkanlayer_pa_k_kernel(
 
         def distance(step):
             n = step // 2
+            done["distance"] = step + 1
             if step % 2 == 0:
                 x_spread.append(bank(4 + n % 3, [P, B], F32, "x_spread"))
                 nc.tensor.matmul(
@@ -263,32 +264,44 @@ def tile_advancedkanlayer_pa_k_kernel(
             outer = dist[:, n : n + 2, :]
             zigzag = slope[:, n : n + 2, :]
             scalar_steps.append(
-                lambda o=inner, i=outer: nc.scalar.activation(out=o[:], in_=i, func=ACT.Relu, bias=1.0, scale=-2.0)
-            )
-            scalar_steps.append(
-                lambda i=outer: nc.scalar.activation(out=i, in_=i, func=ACT.Relu, bias=1.0, scale=-1.0)
-            )
-            scalar_steps.append(
                 lambda z=zigzag: nc.scalar.activation(out=z, in_=z, func=ACT.Abs, bias=minus_one[:], scale=1.0)
             )
             vector_steps.append(
-                lambda o=inner, i=outer: nc.vector.tensor_tensor(out=o[:], in0=o[:], in1=i, op=ALU.add)
+                lambda o=inner, i=outer: nc.vector.tensor_scalar(
+                    out=o[:], in0=i, scalar1=0.5, scalar2=0.5, op0=ALU.min, op1=ALU.subtract
+                )
+            )
+            vector_steps.append(
+                lambda i=outer: nc.vector.tensor_scalar(
+                    out=i, in0=i, scalar1=1.0, scalar2=1.0, op0=ALU.min, op1=ALU.subtract
+                )
+            )
+            vector_steps.append(
+                lambda o=inner, i=outer: nc.vector.scalar_tensor_tensor(
+                    out=o[:], in0=o[:], scalar=2.0, in1=i, op0=ALU.mult, op1=ALU.add
+                )
             )
             vector_steps.append(
                 lambda o=inner, z=zigzag: nc.vector.scalar_tensor_tensor(
                     out=z, in0=z, scalar=0.5, in1=o[:], op0=ALU.subtract, op1=ALU.mult
                 )
             )
+        done = {"distance": 0, "scalar": 0, "vector": 0}
 
-        done = {"scalar": 0, "vector": 0}
-
-        def slope_steps(goal):
-            if done["vector"] < 2 * (done["scalar"] // 3):
-                vector_steps[done["vector"]]()
-                done["vector"] += 1
-            while done["scalar"] < min(goal, len(scalar_steps)):
+        def scalar_slope(most):
+            while done["scalar"] < len(scalar_steps) and most > 0 and done["distance"] >= 4 * done["scalar"] + 4:
                 scalar_steps[done["scalar"]]()
                 done["scalar"] += 1
+                most -= 1
+
+        def vector_slope(most):
+            while done["vector"] < len(vector_steps) and most > 0:
+                pair = done["vector"] // 4
+                if done["distance"] < 4 * pair + 4 or (done["vector"] % 4 == 3 and done["scalar"] <= pair):
+                    break
+                vector_steps[done["vector"]]()
+                done["vector"] += 1
+                most -= 1
 
         early_cols = P * EARLY_GROUPS
         split = order[-SPLIT:]
@@ -324,7 +337,8 @@ def tile_advancedkanlayer_pa_k_kernel(
             if c > 0:
                 quantise_pass(c - 1, g_grouped_before)
             if c in WIDE:
-                slope_steps(done["scalar"] + 1)
+                scalar_slope(1)
+            vector_slope(V_SLOPE[c])
             g_grouped_before = g_grouped
             multiply_base(min(base_next[0] + BASE_RATE, c - 1))
         quantise_pass(PASSES - 1, g_grouped_before)
@@ -346,10 +360,10 @@ def tile_advancedkanlayer_pa_k_kernel(
         spline_rows = keep.tile([P, ROW_TILES, I], F32)
 
         def weigh(n):
-            assert done["vector"] >= 2 * (n // 2 + 1)
+            assert done["vector"] >= 4 * (n // 2 + 1)
             weighted[n] = stream.tile([P, B], F32, tag="weighted", bufs=WEIGHTED_BUFS, name="weighted")
             nc.vector.scalar_tensor_tensor(
-                out=weighted[n][:], in0=h[n][:], scalar=6.0, in1=slope[:, n, :], op0=ALU.mult, op1=ALU.mult
+                out=weighted[n][:], in0=h[n][:], scalar=-6.0, in1=slope[:, n, :], op0=ALU.mult, op1=ALU.mult
             )
 
         def flip_group(n):
@@ -394,24 +408,20 @@ def tile_advancedkanlayer_pa_k_kernel(
         base_part = keep.tile([P, B], F32)
         base_rows = keep.tile([P, ROW_TILES, I], F32)
         regroup_next = -(-(PASSES - FIRST_JOB) // JOBS_PER_CHUNK)
-        columns = 0
-        first_goal = done["scalar"]
         for k in range(ready, len(units)):
             while regroup_next < len(units) and regroup_next <= k + 1:
                 unit = units[regroup_next]
                 width = unit[2] - unit[1]
-                cut = width * VECTOR_SHARE // 32 // RUN // 2 * RUN * 2 if unit not in units[-SPLIT:] else 0
+                share = VECTOR_SHARE if done["vector"] < len(vector_steps) else LATE_SHARE
+                cut = width * share // 32 // RUN // 2 * RUN * 2 if unit not in units[-SPLIT:] else 0
                 if cut > 0:
                     regroup(unit, (0, cut), nc.vector.tensor_copy)
                 regroup(unit, (cut, width), nc.scalar.copy)
                 regroup_next += 1
             unit = units[k]
             quantise_unit(unit)
-            columns += unit[2] - unit[1]
-            if unit in units[-SPLIT:]:
-                slope_steps(done["scalar"] + LATE_RATE)
-            else:
-                slope_steps(first_goal + (EARLY_STEPS - first_goal) * columns // SLOPE_COLS)
+            scalar_slope(1)
+            vector_slope(V_RATE)
             if k == ready:
                 nc.scalar.mul(out=base_part[:], in_=base_bank[:], mul=0.1)
                 base_flipped = bank(7, [P, ROW_TILES, I], F32, "base_flipped")
@@ -433,8 +443,8 @@ def tile_advancedkanlayer_pa_k_kernel(
                 for e in share:
                     early_steps[e]()
 
-        while done["vector"] < len(vector_steps):
-            slope_steps(len(scalar_steps))
+        scalar_slope(len(scalar_steps))
+        vector_slope(len(vector_steps))
         for n in late:
             close_group(n)
         store(early)

@@ -29,12 +29,10 @@ BASE_PASSES = COLS // I
 BASE_CHUNKS = PASSES // BASE_PASSES
 CHUNKS = BASE_CHUNKS + PASSES
 RUN = 4
-LATE_SHARE = 14
-VECTOR_SHARE = 10
+LATE_SHARE = 16
+VECTOR_SHARE = 12
 PIECE = 1024
 SPLIT = 8
-WIDE = (5, 7, 9, 13)
-V_SLOPE = (0, 0, 0, 1, 1, 0, 0, 1, 1, 0, 0, 1, 1, 0, 0, 1)
 V_RATE = 1
 RAW_BUFS = 8
 FIRST_STEPS = 2
@@ -330,15 +328,17 @@ def tile_advancedkanlayer_pa_k_kernel(
         g_grouped_before = None
         for c in range(PASSES):
             g_grouped = flip_pass(c)
-            if FIRST_STEPS + c < 2 * GROUPS:
-                distance(FIRST_STEPS + c)
+            for s in range(1 + c % 2):
+                if done["distance"] < 2 * GROUPS:
+                    distance(done["distance"])
             if c >= FIRST_JOB:
                 jobs[c - FIRST_JOB]()
             if c > 0:
                 quantise_pass(c - 1, g_grouped_before)
-            if c in WIDE:
+            if c % 3 == 0:
                 scalar_slope(1)
-            vector_slope(V_SLOPE[c])
+            else:
+                vector_slope(1)
             g_grouped_before = g_grouped
             multiply_base(min(base_next[0] + BASE_RATE, c - 1))
         quantise_pass(PASSES - 1, g_grouped_before)
@@ -385,11 +385,12 @@ def tile_advancedkanlayer_pa_k_kernel(
             weigh(n)
             flip_group(n)
 
+
         out_rows = keep.tile([P, ROW_TILES, I], F32)
 
-        def store(groups):
+        def store(groups, engine):
             cols = slice(FEATS * groups[0], FEATS * (groups[-1] + 1))
-            nc.vector.tensor_tensor(
+            engine.tensor_tensor(
                 out=out_rows[:, :, cols], in0=spline_rows[:, :, cols], in1=base_rows[:, :, cols], op=ALU.add
             )
             nc.sync.dma_start(
@@ -403,7 +404,7 @@ def tile_advancedkanlayer_pa_k_kernel(
             early_steps.append(lambda n=n: close_group(n))
             if n > 0:
                 early_steps.append(lambda n=n: add_neighbours(n - 1))
-        early_steps.append(lambda: add_neighbours(EARLY_GROUPS - 1))
+        early_steps[-2], early_steps[-1] = early_steps[-1], early_steps[-2]
 
         base_part = keep.tile([P, B], F32)
         base_rows = keep.tile([P, ROW_TILES, I], F32)
@@ -447,7 +448,7 @@ def tile_advancedkanlayer_pa_k_kernel(
         vector_slope(len(vector_steps))
         for n in late:
             close_group(n)
-        store(early)
-        for n in late:
+        store(early[:-1], nc.gpsimd)
+        for n in range(EARLY_GROUPS - 1, GROUPS):
             add_neighbours(n)
-        store(late)
+        store(range(EARLY_GROUPS - 1, GROUPS), nc.vector)

@@ -147,8 +147,8 @@ def tile_advancedkanlayer_pa_k_kernel(
         half_knot = const.tile([P, 1], F32)
         nc.vector.tensor_scalar(out=half_knot[:], in0=neg_knot[:], scalar1=0.5, scalar2=None, op0=ALU.add)
 
-        g_codes = keep.tile([P, PASSES, B], U32, align_bytes=64)
-        g_scales = keep.tile([P, PASSES, B], U8, align_bytes=64)
+        g_codes = keep.tile([P, PASSES, B], U32, align_bytes=256)
+        g_scales = keep.tile([P, PASSES, B], U8, align_bytes=256)
         dist = keep.tile([P, GROUPS, B], F32)
         slope = keep.tile([P, GROUPS, B], F32)
         x_spread = []
@@ -228,8 +228,8 @@ def tile_advancedkanlayer_pa_k_kernel(
         def quantise_unit(unit):
             j, first, last = unit
             width = last - first
-            words = stream.tile([P, COLS], U32, tag="codes", bufs=6, align_bytes=64, name="words")
-            scales = stream.tile([P, COLS], U8, tag="scales", bufs=6, align_bytes=64, name="scales")
+            words = stream.tile([P, COLS], U32, tag="codes", bufs=6, align_bytes=256, name="words")
+            scales = stream.tile([P, COLS], U8, tag="scales", bufs=6, align_bytes=256, name="scales")
             begin = 0
             while begin < width:
                 end = begin + PIECE
@@ -314,6 +314,16 @@ def tile_advancedkanlayer_pa_k_kernel(
 
         base_bank = bank(7, [P, B], F32, "base_bank")
 
+        h = {}
+        multiplied = set()
+
+        def multiply_unit(unit, groups):
+            j, first, last = unit
+            for n in groups:
+                if first <= P * n < last and (j, n) not in multiplied:
+                    multiply(h[n], unit, P * n - first, j - BASE_CHUNKS)
+                    multiplied.add((j, n))
+
         base_next = [0]
 
         def multiply_base(most):
@@ -341,19 +351,22 @@ def tile_advancedkanlayer_pa_k_kernel(
                 vector_slope(1)
             g_grouped_before = g_grouped
             multiply_base(min(base_next[0] + BASE_RATE, c - 1))
+            if done["distance"] == 2 * GROUPS and c % 2 == 1:
+                for n in range(4, 7):
+                    if n not in h:
+                        h[n] = bank(n, [P, B], F32, "h%d" % n)
+                for unit in units:
+                    if unit[0] >= BASE_CHUNKS and unit in codes and unit[0] - BASE_CHUNKS < c - 1:
+                        multiply_unit(unit, range(4, 7))
         quantise_pass(PASSES - 1, g_grouped_before)
         if (PASSES - FIRST_JOB) % JOBS_PER_CHUNK == 1:
             jobs[PASSES - FIRST_JOB]()
         ready = (PASSES - FIRST_JOB) // JOBS_PER_CHUNK
 
         multiply_base(PASSES)
-        h = [bank(n, [P, B], F32, "h%d" % n) for n in range(GROUPS - 1)]
-
-        def multiply_unit(unit, groups):
-            j, first, last = unit
-            for n in groups:
-                if first <= P * n < last:
-                    multiply(h[n], unit, P * n - first, j - BASE_CHUNKS)
+        for n in range(GROUPS - 1):
+            if n not in h:
+                h[n] = bank(n, [P, B], F32, "h%d" % n)
 
         weighted = {}
         flat = {}
@@ -434,7 +447,7 @@ def tile_advancedkanlayer_pa_k_kernel(
                 before = [u for u in units[:ready] if u[0] >= BASE_CHUNKS]
                 for u in before:
                     multiply_unit(u, range(GROUPS - 1))
-                h.append(bank(7, [P, B], F32, "h7"))
+                h[GROUPS - 1] = bank(7, [P, B], F32, "h7")
                 for u in before:
                     multiply_unit(u, range(GROUPS - 1, GROUPS))
             multiply_unit(unit, range(GROUPS))

@@ -62,8 +62,9 @@ def tile_advancedkanlayer_pa_k_kernel(
         def bank(n, shape, dtype, name):
             return psum.tile(shape, dtype, tag="bank%d" % n, name=name)
 
-        knots = const.tile([P, G], BF16)
-        nc.scalar.dma_start(out=knots[:], in_=grid_points.partition_broadcast(P))
+        knot_row = const.tile([P, G], BF16)
+        nc.vector.memset(knot_row[:], 0.0)
+        nc.scalar.dma_start(out=knot_row[0:1, :], in_=grid_points.rearrange("(o g) -> o g", o=1))
         spark = const.tile([P, 1], F32)
         nc.vector.memset(spark[:], 0.0)
         nc.scalar.activation(out=spark[:], in_=spark[:], func=ACT.Abs)
@@ -124,12 +125,22 @@ def tile_advancedkanlayer_pa_k_kernel(
             out=spread[:].rearrange("p (i g) -> p i g", g=G),
             in_=ident_bf16[:].unsqueeze(2).to_broadcast([P, P, G]),
         )
-        same_knot = const.tile([P, G], F32)
-        nc.vector.tensor_reduce(
-            out=same_knot[:],
-            in_=ident_f32[:].rearrange("p (j g) -> p g j", g=G),
-            axis=AXIS_X,
-            op=ALU.add,
+        ones = const.tile([P, G], BF16)
+        nc.vector.memset(ones[:], 1.0)
+        knot_columns = const.tile([P, P], BF16)
+        nc.vector.tensor_copy(
+            out=knot_columns[:].rearrange("p (j g) -> p j g", g=G),
+            in_=knot_row[:].unsqueeze(1).to_broadcast([P, FEATS, G]),
+        )
+        knot_bank = bank(6, [P, G], F32, "knot_bank")
+        nc.tensor.matmul(out=knot_bank[:], lhsT=knot_columns[:], rhs=ones[:], start=True, stop=True)
+        neg_knot = const.tile([P, 1], F32)
+        nc.vector.tensor_scalar(
+            out=neg_knot[:], in0=knot_bank[:, 0:1], scalar1=-1.0, scalar2=None, op0=ALU.mult
+        )
+        half_knot = const.tile([P, 1], F32)
+        nc.vector.tensor_scalar(
+            out=half_knot[:], in0=knot_bank[:, 0:1], scalar1=-1.0, scalar2=0.5, op0=ALU.mult, op1=ALU.add
         )
         xT_bank = bank(7, [P, B], BF16, "xT_bank")
         for r in range(ROW_TILES):
@@ -138,14 +149,6 @@ def tile_advancedkanlayer_pa_k_kernel(
             )
         xT = const.tile([P, B], BF16)
         nc.vector.tensor_copy(out=xT[:], in_=xT_bank[:])
-        own_knot = const.tile([P, G], F32)
-        nc.vector.scalar_tensor_tensor(
-            out=own_knot[:], in0=same_knot[:], scalar=-1.0, in1=knots[:], op0=ALU.mult, op1=ALU.mult
-        )
-        neg_knot = const.tile([P, 1], F32)
-        nc.vector.tensor_reduce(out=neg_knot[:], in_=own_knot[:], axis=AXIS_X, op=ALU.add)
-        half_knot = const.tile([P, 1], F32)
-        nc.vector.tensor_scalar(out=half_knot[:], in0=neg_knot[:], scalar1=0.5, scalar2=None, op0=ALU.add)
 
         g_codes = keep.tile([P, PASSES, B], U32, align_bytes=256)
         g_scales = keep.tile([P, PASSES, B], U8, align_bytes=256)

@@ -29,8 +29,8 @@ BASE_PASSES = COLS // I
 BASE_CHUNKS = PASSES // BASE_PASSES
 CHUNKS = BASE_CHUNKS + PASSES
 RUN = 4
-LATE_SHARE = 16
-VECTOR_SHARE = 12
+LATE_SHARE = 15
+VECTOR_SHARE = 11
 PIECE = 1024
 SPLIT = 8
 V_RATE = 1
@@ -64,13 +64,13 @@ def tile_advancedkanlayer_pa_k_kernel(
 
         knot_row = const.tile([P, G], BF16)
         nc.vector.memset(knot_row[:], 0.0)
-        nc.scalar.dma_start(out=knot_row[0:1, :], in_=grid_points.rearrange("(o g) -> o g", o=1))
         spark = const.tile([P, 1], F32)
         nc.vector.memset(spark[:], 0.0)
         nc.scalar.activation(out=spark[:], in_=spark[:], func=ACT.Abs)
         minus_one = const.tile([P, 1], F32)
         nc.vector.memset(minus_one[:], -1.0)
 
+        nc.sync.dma_start(out=knot_row[0:1, :], in_=grid_points.rearrange("(o g) -> o g", o=1))
         x_rows = const.tile([P, ROW_TILES, I], BF16)
         nc.sync.dma_start(out=x_rows[:], in_=x_norm.rearrange("(r p) i -> p r i", p=P))
 

@@ -29,7 +29,8 @@ BASE_PASSES = COLS // I
 BASE_CHUNKS = PASSES // BASE_PASSES
 CHUNKS = BASE_CHUNKS + PASSES
 RUN = 4
-LATE_SHARE = 15
+TREE = 3
+LATE_SHARE = 14
 VECTOR_SHARE = 11
 PIECE = 1024
 SPLIT = 8
@@ -70,9 +71,9 @@ def tile_advancedkanlayer_pa_k_kernel(
         minus_one = const.tile([P, 1], F32)
         nc.vector.memset(minus_one[:], -1.0)
 
-        nc.sync.dma_start(out=knot_row[0:1, :], in_=grid_points.rearrange("(o g) -> o g", o=1))
         x_rows = const.tile([P, ROW_TILES, I], BF16)
         nc.sync.dma_start(out=x_rows[:], in_=x_norm.rearrange("(r p) i -> p r i", p=P))
+        nc.sync.dma_start(out=knot_row[0:1, :], in_=grid_points.rearrange("(o g) -> o g", o=1))
 
         base_rows_in = base_activation.rearrange("(c p t) i -> p c (t i)", p=P, t=PACK)
         w_rows_in = spline_weight.rearrange("(c p t) i g -> c p (t i g)", p=P, t=PACK)
@@ -127,6 +128,13 @@ def tile_advancedkanlayer_pa_k_kernel(
         )
         ones = const.tile([P, G], BF16)
         nc.vector.memset(ones[:], 1.0)
+        xT_bank = bank(7, [P, B], BF16, "xT_bank")
+        for r in range(ROW_TILES):
+            nc.tensor.transpose(
+                out=xT_bank[:, P * r : P * (r + 1)], in_=x_rows[:, r, :], identity=ident_bf16[:]
+            )
+        xT = const.tile([P, B], BF16)
+        nc.vector.tensor_copy(out=xT[:], in_=xT_bank[:])
         knot_columns = const.tile([P, P], BF16)
         nc.vector.tensor_copy(
             out=knot_columns[:].rearrange("p (j g) -> p j g", g=G),
@@ -142,13 +150,6 @@ def tile_advancedkanlayer_pa_k_kernel(
         nc.vector.tensor_scalar(
             out=half_knot[:], in0=knot_bank[:, 0:1], scalar1=-1.0, scalar2=0.5, op0=ALU.mult, op1=ALU.add
         )
-        xT_bank = bank(7, [P, B], BF16, "xT_bank")
-        for r in range(ROW_TILES):
-            nc.tensor.transpose(
-                out=xT_bank[:, P * r : P * (r + 1)], in_=x_rows[:, r, :], identity=ident_bf16[:]
-            )
-        xT = const.tile([P, B], BF16)
-        nc.vector.tensor_copy(out=xT[:], in_=xT_bank[:])
 
         g_codes = keep.tile([P, PASSES, B], U32, align_bytes=256)
         g_scales = keep.tile([P, PASSES, B], U8, align_bytes=256)
@@ -401,6 +402,19 @@ def tile_advancedkanlayer_pa_k_kernel(
             weigh(n)
             flip_group(n)
 
+        def tree(n):
+            eights = stream.tile([P, ROW_TILES, FEATS, G], F32, tag="eights", bufs=2, name="eights")
+            nc.scalar.copy(out=eights[:].rearrange("p r j g -> p r (j g)"), in_=flat[n][:])
+            nc.gpsimd.tensor_tensor(
+                out=eights[:, :, :, 0:4], in0=eights[:, :, :, 0:4], in1=eights[:, :, :, 4:8], op=ALU.add
+            )
+            nc.gpsimd.tensor_tensor(
+                out=eights[:, :, :, 0:2], in0=eights[:, :, :, 0:2], in1=eights[:, :, :, 2:4], op=ALU.add
+            )
+            nc.gpsimd.tensor_tensor(
+                out=spline_rows[:, :, FEATS * n : FEATS * (n + 1)], in0=eights[:, :, :, 0], in1=eights[:, :, :, 1], op=ALU.add
+            )
+
 
         out_rows = keep.tile([P, ROW_TILES, I], F32)
 
@@ -419,7 +433,7 @@ def tile_advancedkanlayer_pa_k_kernel(
         for n in early:
             early_steps.append(lambda n=n: close_group(n))
             if n > 0:
-                early_steps.append(lambda n=n: add_neighbours(n - 1))
+                early_steps.append(lambda n=n: (tree if n - 1 == TREE else add_neighbours)(n - 1))
         early_steps[-2], early_steps[-1] = early_steps[-1], early_steps[-2]
 
         base_part = keep.tile([P, B], F32)

from contextlib import ExitStack

import concourse.mybir as mybir
from concourse.masks import make_identity

F32 = mybir.dt.float32
BF16 = mybir.dt.bfloat16
U32 = mybir.dt.uint32
U8 = mybir.dt.uint8
E4M3_X4 = mybir.dt.float8_e4m3fn_x4
E5M2_X4 = mybir.dt.float8_e5m2_x4
ALU = mybir.AluOpType
ACT = mybir.ActivationFunctionType
AXIS_X = mybir.AxisListType.X

P = 128
PACK = 4
K_PASS = P * PACK

B, I, O, G = 512, 128, 8192, 8
COLS = I * G
PASSES = O // K_PASS
GROUPS = COLS // P
FEATS = P // G
ROW_TILES = B // P
BLOCK_PASSES = 2
BLOCKS = PASSES // BLOCK_PASSES
BASE_PASSES = COLS // I
BASE_CHUNKS = PASSES // BASE_PASSES
CHUNKS = BASE_CHUNKS + PASSES
RUN = 4
TREE = 3
LATE_SHARE = 14
VECTOR_SHARE = 11
PIECE = 1024
SPLIT = 8
V_RATE = 1
RAW_BUFS = 8
FIRST_STEPS = 2
FIRST_JOB = 3
EARLY_GROUPS = 6
BASE_RATE = 2
BASE_AFTER = 2
WEIGHTED_BUFS = 2
G_BUFS = 2
HELP = 2
JOBS_PER_CHUNK = 3

FLOPS = 2 * B * O * (COLS + I)


def tile_advancedkanlayer_pa_k_kernel(
    tc, x_norm, spline_weight, base_activation, grid_points, grad_out, out
):
    nc = tc.nc
    with ExitStack() as ctx:
        const = ctx.enter_context(tc.tile_pool(name="const", bufs=1))
        keep = ctx.enter_context(tc.tile_pool(name="keep", bufs=1))
        stream = ctx.enter_context(tc.tile_pool(name="stream", bufs=2))
        psum = ctx.enter_context(tc.psum_pool(name="psum", bufs=1))
        ctx.enter_context(tc.manual_schedule())

        def bank(n, shape, dtype, name):
            return psum.tile(shape, dtype, tag="bank%d" % n, name=name)

        knot_row = const.tile([P, G], BF16)
        nc.vector.memset(knot_row[:], 0.0)
        spark = const.tile([P, 1], F32)
        nc.vector.memset(spark[:], 0.0)
        nc.scalar.activation(out=spark[:], in_=spark[:], func=ACT.Abs)
        minus_one = const.tile([P, 1], F32)
        nc.vector.memset(minus_one[:], -1.0)

        x_rows = const.tile([P, ROW_TILES, I], BF16)
        nc.sync.dma_start(out=x_rows[:], in_=x_norm.rearrange("(r p) i -> p r i", p=P))
        nc.sync.dma_start(out=knot_row[0:1, :], in_=grid_points.rearrange("(o g) -> o g", o=1))

        base_rows_in = base_activation.rearrange("(c p t) i -> p c (t i)", p=P, t=PACK)
        w_rows_in = spline_weight.rearrange("(c p t) i g -> c p (t i g)", p=P, t=PACK)
        block_cols = BLOCK_PASSES * K_PASS
        needs = [(BLOCK_PASSES * k, 0, k) for k in range(BLOCKS)]
        base_chunks = list(range(BASE_CHUNKS))
        spline_chunks = list(range(BASE_CHUNKS, CHUNKS))
        order = spline_chunks[:BASE_AFTER] + base_chunks + spline_chunks[BASE_AFTER:]
        needs += [(FIRST_JOB + JOBS_PER_CHUNK * s, 1, order[s]) for s in range(CHUNKS)]
        needs.sort()
        loaded = {}
        waiting = list(needs)

        def load_next():
            if not waiting:
                return
            need, kind, k = waiting[0]
            waiting.remove(waiting[0])
            raw = stream.tile([P, PACK * COLS], BF16, tag="raw", bufs=RAW_BUFS, name="raw")
            loaded[(kind, k)] = raw
            if kind == 0:
                dst = raw[:].rearrange("p (r o) -> p r o", r=ROW_TILES)
                src = grad_out[:, block_cols * k : block_cols * (k + 1)].rearrange(
                    "(r p) o -> p r o", p=P
                )
                pieces = BLOCK_PASSES if k == 0 else 1
                width = block_cols // pieces
                for s in range(pieces):
                    nc.sync.dma_start(
                        out=dst[:, :, width * s : width * (s + 1)], in_=src[:, :, width * s : width * (s + 1)]
                    )
            elif k < BASE_CHUNKS:
                nc.sync.dma_start(
                    out=raw[:].rearrange("p (c w) -> p c w", c=BASE_PASSES),
                    in_=base_rows_in[:, BASE_PASSES * k : BASE_PASSES * (k + 1), :],
                )
            else:
                nc.sync.dma_start(out=raw[:], in_=w_rows_in[k - BASE_CHUNKS])

        for n in range(RAW_BUFS):
            load_next()

        ident_bf16 = const.tile([P, P], BF16)
        make_identity(nc, ident_bf16[:])
        ident_f32 = const.tile([P, P], F32)
        make_identity(nc, ident_f32[:])

        spread = const.tile([P, COLS], BF16)
        nc.vector.tensor_copy(
            out=spread[:].rearrange("p (i g) -> p i g", g=G),
            in_=ident_bf16[:].unsqueeze(2).to_broadcast([P, P, G]),
        )
        ones = const.tile([P, G], BF16)
        nc.vector.memset(ones[:], 1.0)
        xT_bank = bank(7, [P, B], BF16, "xT_bank")
        for r in range(ROW_TILES):
            nc.tensor.transpose(
                out=xT_bank[:, P * r : P * (r + 1)], in_=x_rows[:, r, :], identity=ident_bf16[:]
            )
        xT = const.tile([P, B], BF16)
        nc.vector.tensor_copy(out=xT[:], in_=xT_bank[:])
        knot_columns = const.tile([P, P], BF16)
        nc.vector.tensor_copy(
            out=knot_columns[:].rearrange("p (j g) -> p j g", g=G),
            in_=knot_row[:].unsqueeze(1).to_broadcast([P, FEATS, G]),
        )
        knot_bank = bank(6, [P, G], F32, "knot_bank")
        nc.tensor.matmul(out=knot_bank[:], lhsT=knot_columns[:], rhs=ones[:], start=True, stop=True)
        neg_knot = const.tile([P, 1], F32)
        nc.vector.tensor_scalar(
            out=neg_knot[:], in0=knot_bank[:, 0:1], scalar1=-1.0, scalar2=None, op0=ALU.mult
        )
        half_knot = const.tile([P, 1], F32)
        nc.vector.tensor_scalar(
            out=half_knot[:], in0=knot_bank[:, 0:1], scalar1=-1.0, scalar2=0.5, op0=ALU.mult, op1=ALU.add
        )

        g_codes = keep.tile([P, PASSES, B], U32, align_bytes=256)
        g_scales = keep.tile([P, PASSES, B], U8, align_bytes=256)
        dist = keep.tile([P, GROUPS, B], F32)
        slope = keep.tile([P, GROUPS, B], F32)
        x_spread = []

        def distance(step):
            n = step // 2
            done["distance"] = step + 1
            if step % 2 == 0:
                x_spread.append(bank(4 + n % 3, [P, B], F32, "x_spread"))
                nc.tensor.matmul(
                    out=x_spread[n][:], lhsT=spread[:, P * n : P * (n + 1)], rhs=xT[:], start=True, stop=True
                )
                nc.scalar.activation(
                    out=dist[:, n, :], in_=x_spread[n][:], func=ACT.Abs, bias=neg_knot[:], scale=1.0
                )
            else:
                nc.scalar.activation(
                    out=slope[:, n, :], in_=x_spread[n][:], func=ACT.Abs, bias=half_knot[:], scale=1.0
                )

        def flip_pass(c):
            words = loaded[(0, c // BLOCK_PASSES)][:].bitcast(F32).rearrange("p (r w) -> p r w", r=ROW_TILES)
            first_word = (K_PASS // 2) * (c % BLOCK_PASSES)
            g_grouped = stream.tile([P, B * PACK], BF16, tag="g_grouped", bufs=G_BUFS, align_bytes=64)
            g_grouped_words = g_grouped[:].bitcast(F32).rearrange("p (b u) -> p b u", u=2)
            for half in range(2):
                flipped = bank((2 * c + half) % 4, [P, 2, B // 2], F32, "flipped")
                for u in range(2):
                    for r in range(2):
                        nc.tensor.transpose(
                            out=flipped[:, u, P * r : P * (r + 1)],
                            in_=words[:, 2 * half + r, first_word + u : first_word + 2 * P : 2],
                            identity=ident_f32[:],
                        )
                copy_out = nc.vector.tensor_copy if half == 1 and c < HELP else nc.scalar.copy
                copy_out(
                    out=g_grouped_words[:, (B // 2) * half : (B // 2) * (half + 1), :],
                    in_=flipped[:].rearrange("p u b -> p b u"),
                )
            if c % BLOCK_PASSES == BLOCK_PASSES - 1:
                load_next()
            return g_grouped

        def quantise_pass(c, g_grouped):
            nc.vector.quantize_mx(
                out=g_codes[:, c, :].bitcast(E5M2_X4), scales=g_scales[:, c, :], in_=g_grouped[:]
            )

        grouped = {}
        regrouped = {}

        def regroup(unit, share, copy):
            j, first, last = unit
            if unit not in grouped:
                grouped[unit] = stream.tile(
                    [P, COLS, PACK], BF16, tag="grouped", bufs=3, align_bytes=64, name="grouped"
                )
            begin, end = share
            if j < BASE_CHUNKS:
                src = loaded[(1, j)][:].rearrange("p (c t k r) -> p c k t r", c=BASE_PASSES, t=PACK, r=RUN)
                dst = grouped[unit][:].rearrange("p (c k r) t -> p c k t r", c=BASE_PASSES, r=RUN)
                step = I
            else:
                src = loaded[(1, j)][:].rearrange("p (t k r) -> p k t r", t=PACK, r=RUN)
                dst = grouped[unit][:].rearrange("p (k r) t -> p k t r", r=RUN)
                step = RUN
            copy(
                out=dst[:, begin // step : end // step],
                in_=src[:, (first + begin) // step : (first + end) // step],
            )
            regrouped[j] = regrouped.get(j, 0) + end - begin
            if regrouped[j] == COLS:
                load_next()

        codes = {}

        def quantise_unit(unit):
            j, first, last = unit
            width = last - first
            words = stream.tile([P, COLS], U32, tag="codes", bufs=6, align_bytes=256, name="words")
            scales = stream.tile([P, COLS], U8, tag="scales", bufs=6, align_bytes=256, name="scales")
            begin = 0
            while begin < width:
                end = begin + PIECE
                while end > width:
                    end = begin + (end - begin) // 2
                nc.vector.quantize_mx(
                    out=words[:, begin:end].bitcast(E4M3_X4),
                    scales=scales[:, begin:end],
                    in_=grouped[unit][:].rearrange("p w t -> p (w t)")[:, PACK * begin : PACK * end],
                )
                begin = end
            codes[unit] = (words, scales)

        def multiply(acc, unit, column, c):
            words, scales = codes[unit]
            nc.tensor.matmul_mx(
                out=acc[:],
                lhsT=words[:, column : column + P].bitcast(E4M3_X4),
                lhsT_scale=scales[:, column : column + P],
                rhs=g_codes[:, c, :].bitcast(E5M2_X4),
                rhs_scale=g_scales[:, c, :],
                start=(c == 0),
                stop=(c == PASSES - 1),
            )

        scalar_steps = []
        vector_steps = []
        for n in range(0, GROUPS, 2):
            inner = keep.tile([P, 2, B], F32, tag="inner", bufs=2, name="inner")
            outer = dist[:, n : n + 2, :]
            zigzag = slope[:, n : n + 2, :]
            scalar_steps.append(
                lambda z=zigzag: nc.scalar.activation(out=z, in_=z, func=ACT.Abs, bias=minus_one[:], scale=1.0)
            )
            vector_steps.append(
                lambda o=inner, i=outer: nc.vector.tensor_scalar(
                    out=o[:], in0=i, scalar1=0.5, scalar2=0.5, op0=ALU.min, op1=ALU.subtract
                )
            )
            vector_steps.append(
                lambda i=outer: nc.vector.tensor_scalar(
                    out=i, in0=i, scalar1=1.0, scalar2=1.0, op0=ALU.min, op1=ALU.subtract
                )
            )
            vector_steps.append(
                lambda o=inner, i=outer: nc.vector.scalar_tensor_tensor(
                    out=o[:], in0=o[:], scalar=2.0, in1=i, op0=ALU.mult, op1=ALU.add
                )
            )
            vector_steps.append(
                lambda o=inner, z=zigzag: nc.vector.scalar_tensor_tensor(
                    out=z, in0=z, scalar=0.5, in1=o[:], op0=ALU.subtract, op1=ALU.mult
                )
            )
        done = {"distance": 0, "scalar": 0, "vector": 0}

        def scalar_slope(most):
            while done["scalar"] < len(scalar_steps) and most > 0 and done["distance"] >= 4 * done["scalar"] + 4:
                scalar_steps[done["scalar"]]()
                done["scalar"] += 1
                most -= 1

        def vector_slope(most):
            while done["vector"] < len(vector_steps) and most > 0:
                pair = done["vector"] // 4
                if done["distance"] < 4 * pair + 4 or (done["vector"] % 4 == 3 and done["scalar"] <= pair):
                    break
                vector_steps[done["vector"]]()
                done["vector"] += 1
                most -= 1

        early_cols = P * EARLY_GROUPS
        split = order[-SPLIT:]
        units = [(j, 0, COLS) for j in order[:-SPLIT]]
        units += [(j, 0, early_cols) for j in split]
        units += [(j, early_cols, COLS) for j in split]
        jobs = []
        for unit in units:
            jobs.append(lambda u=unit: regroup(u, (0, COLS // 2), nc.vector.tensor_copy))
            jobs.append(lambda u=unit: regroup(u, (COLS // 2, COLS), nc.vector.tensor_copy))
            jobs.append(lambda u=unit: quantise_unit(u))

        base_bank = bank(7, [P, B], F32, "base_bank")

        h = {}
        multiplied = set()

        def multiply_unit(unit, groups):
            j, first, last = unit
            for n in groups:
                if first <= P * n < last and (j, n) not in multiplied:
                    multiply(h[n], unit, P * n - first, j - BASE_CHUNKS)
                    multiplied.add((j, n))

        base_next = [0]

        def multiply_base(most):
            c = base_next[0]
            while c < most and (c // BASE_PASSES, 0, COLS) in codes:
                multiply(base_bank, (c // BASE_PASSES, 0, COLS), I * (c % BASE_PASSES), c)
                c += 1
            base_next[0] = c

        for step in range(FIRST_STEPS):
            distance(step)
        g_grouped_before = None
        for c in range(PASSES):
            g_grouped = flip_pass(c)
            for s in range(1 + c % 2):
                if done["distance"] < 2 * GROUPS:
                    distance(done["distance"])
            if c >= FIRST_JOB:
                jobs[c - FIRST_JOB]()
            if c > 0:
                quantise_pass(c - 1, g_grouped_before)
            if c % 3 == 0:
                scalar_slope(1)
            else:
                vector_slope(1)
            g_grouped_before = g_grouped
            multiply_base(min(base_next[0] + BASE_RATE, c - 1))
            if done["distance"] == 2 * GROUPS and c % 2 == 1:
                for n in range(4, 7):
                    if n not in h:
                        h[n] = bank(n, [P, B], F32, "h%d" % n)
                for unit in units:
                    if unit[0] >= BASE_CHUNKS and unit in codes and unit[0] - BASE_CHUNKS < c - 1:
                        multiply_unit(unit, range(4, 7))
        quantise_pass(PASSES - 1, g_grouped_before)
        if (PASSES - FIRST_JOB) % JOBS_PER_CHUNK == 1:
            jobs[PASSES - FIRST_JOB]()
        ready = (PASSES - FIRST_JOB) // JOBS_PER_CHUNK

        multiply_base(PASSES)
        for n in range(GROUPS - 1):
            if n not in h:
                h[n] = bank(n, [P, B], F32, "h%d" % n)

        weighted = {}
        flat = {}
        spline_rows = keep.tile([P, ROW_TILES, I], F32)

        def weigh(n):
            assert done["vector"] >= 4 * (n // 2 + 1)
            weighted[n] = stream.tile([P, B], F32, tag="weighted", bufs=WEIGHTED_BUFS, name="weighted")
            nc.vector.scalar_tensor_tensor(
                out=weighted[n][:], in0=h[n][:], scalar=-6.0, in1=slope[:, n, :], op0=ALU.mult, op1=ALU.mult
            )

        def flip_group(n):
            flat[n] = bank(n, [P, ROW_TILES, P], F32, "flat")
            for r in range(ROW_TILES):
                nc.tensor.transpose(
                    out=flat[n][:, r, :], in_=weighted[n][:, P * r : P * (r + 1)], identity=ident_f32[:]
                )

        def add_neighbours(n):
            nc.vector.tensor_reduce(
                out=spline_rows[:, :, FEATS * n : FEATS * (n + 1)],
                in_=flat[n][:].rearrange("p r (j g) -> p r j g", g=G),
                axis=AXIS_X,
                op=ALU.add,
            )

        def close_group(n):
            weigh(n)
            flip_group(n)

        def tree(n):
            eights = stream.tile([P, ROW_TILES, FEATS, G], F32, tag="eights", bufs=2, name="eights")
            nc.scalar.copy(out=eights[:].rearrange("p r j g -> p r (j g)"), in_=flat[n][:])
            nc.gpsimd.tensor_tensor(
                out=eights[:, :, :, 0:4], in0=eights[:, :, :, 0:4], in1=eights[:, :, :, 4:8], op=ALU.add
            )
            nc.gpsimd.tensor_tensor(
                out=eights[:, :, :, 0:2], in0=eights[:, :, :, 0:2], in1=eights[:, :, :, 2:4], op=ALU.add
            )
            nc.gpsimd.tensor_tensor(
                out=spline_rows[:, :, FEATS * n : FEATS * (n + 1)], in0=eights[:, :, :, 0], in1=eights[:, :, :, 1], op=ALU.add
            )


        out_rows = keep.tile([P, ROW_TILES, I], F32)

        def store(groups, engine):
            cols = slice(FEATS * groups[0], FEATS * (groups[-1] + 1))
            engine.tensor_tensor(
                out=out_rows[:, :, cols], in0=spline_rows[:, :, cols], in1=base_rows[:, :, cols], op=ALU.add
            )
            nc.sync.dma_start(
                out=out.rearrange("(r p) i -> p r i", p=P)[:, :, cols], in_=out_rows[:, :, cols]
            )

        early = range(EARLY_GROUPS)
        late = range(EARLY_GROUPS, GROUPS)
        early_steps = []
        for n in early:
            early_steps.append(lambda n=n: close_group(n))
            if n > 0:
                early_steps.append(lambda n=n: (tree if n - 1 == TREE else add_neighbours)(n - 1))
        early_steps[-2], early_steps[-1] = early_steps[-1], early_steps[-2]

        base_part = keep.tile([P, B], F32)
        base_rows = keep.tile([P, ROW_TILES, I], F32)
        regroup_next = -(-(PASSES - FIRST_JOB) // JOBS_PER_CHUNK)
        for k in range(ready, len(units)):
            while regroup_next < len(units) and regroup_next <= k + 1:
                unit = units[regroup_next]
                width = unit[2] - unit[1]
                share = VECTOR_SHARE if done["vector"] < len(vector_steps) else LATE_SHARE
                cut = width * share // 32 // RUN // 2 * RUN * 2 if unit not in units[-SPLIT:] else 0
                if cut > 0:
                    regroup(unit, (0, cut), nc.vector.tensor_copy)
                regroup(unit, (cut, width), nc.scalar.copy)
                regroup_next += 1
            unit = units[k]
            quantise_unit(unit)
            scalar_slope(1)
            vector_slope(V_RATE)
            if k == ready:
                nc.scalar.mul(out=base_part[:], in_=base_bank[:], mul=0.1)
                base_flipped = bank(7, [P, ROW_TILES, I], F32, "base_flipped")
                for r in range(ROW_TILES):
                    nc.tensor.transpose(
                        out=base_flipped[:, r, :], in_=base_part[:, P * r : P * (r + 1)], identity=ident_f32[:]
                    )
                nc.scalar.copy(out=base_rows[:], in_=base_flipped[:])
                before = [u for u in units[:ready] if u[0] >= BASE_CHUNKS]
                for u in before:
                    multiply_unit(u, range(GROUPS - 1))
                h[GROUPS - 1] = bank(7, [P, B], F32, "h7")
                for u in before:
                    multiply_unit(u, range(GROUPS - 1, GROUPS))
            multiply_unit(unit, range(GROUPS))
            if unit in units[-SPLIT:]:
                s = units[-SPLIT:].index(unit)
                share = range(len(early_steps) * s // SPLIT, len(early_steps) * (s + 1) // SPLIT)
                for e in share:
                    early_steps[e]()

        scalar_slope(len(scalar_steps))
        vector_slope(len(vector_steps))
        for n in late:
            close_group(n)
        store(early[:-1], nc.gpsimd)
        for n in range(EARLY_GROUPS - 1, GROUPS):
            add_neighbours(n)
        store(range(EARLY_GROUPS - 1, GROUPS), nc.vector)
